import numpy as np
import ml_dtypes


def mxq(x, axis, fmt="e4m3"):
    dtype, down = {"e4m3": (ml_dtypes.float8_e4m3fn, 7), "e5m2": (ml_dtypes.float8_e5m2, 14)}[fmt]
    v = np.moveaxis(np.asarray(x, np.float32).astype(ml_dtypes.bfloat16).astype(np.float64), axis, -1)
    blocks = v.reshape(v.shape[:-1] + (-1, 32))
    amax = np.abs(blocks).max(-1, keepdims=True)
    byte = np.maximum(np.where(amax > 0, np.frexp(amax)[1] - 1 + 127, 0) - down, 1)
    scale = np.exp2(byte - 127.0)
    codes = (blocks / scale).astype(np.float32).astype(dtype).astype(np.float64)
    return np.moveaxis((codes * scale).reshape(v.shape), -1, axis)


WIDE = False


def mx_kscale(k):
    if not WIDE:
        return np.ones(k)
    levels = np.array([10, -10, 5, -5, 0])
    a = np.random.permutation(np.resize(levels, k // 512 * 4)).reshape(k // 512, 4)
    idx = np.arange(k)
    return np.exp2(a[idx // 512, idx % 128 // 32])


BF16 = ml_dtypes.bfloat16


def bf(x):
    return np.asarray(x, np.float32).astype(BF16)


def f64(x):
    return np.asarray(x).astype(np.float64)


B, C, H, W, K, O = 1, 512, 32, 32, 3, 512
P = C * K * K
PAD = 1
G = 32


def im2col(a):
    a_pad = np.pad(a, ((0, 0), (0, 0), (PAD, PAD), (PAD, PAD)), mode="reflect")
    cols = np.stack([a_pad[:, :, kh:kh + H, kw:kw + W] for kh in range(K) for kw in range(K)], axis=2)
    cols = cols.reshape(B, P, H * W)
    return np.swapaxes(cols, 1, 2)


def setup_inputs():
    u = np.unique(mx_kscale(P))
    t = u[np.arange(C // G) % len(u)]
    sc = np.repeat(t, G).reshape(1, C, 1, 1)
    sp = np.repeat(t, G * K * K).reshape(P, 1)
    lam = 1.0 if len(u) == 1 else 0.0
    g = 2.0 ** np.round(0.5 * np.log2(np.mean(t ** 2)))
    amp = 0.5 + 1.5 * np.random.random_sample((B, 1, H, W))
    off = 0.6 + 0.4 * np.random.standard_normal((B, 1, H, W))
    bound = np.sqrt(6.0 / P)
    z = np.random.standard_normal((B, C, H, W))
    z[:, 1::2] = lam * z[:, 1::2] - (1.0 - lam) * z[:, 0::2]
    return {"a": bf((z * amp + off * lam) * sc),
            "conv_kernel": bf(np.random.uniform(-bound, bound, (P, O)) * g / sp)}


def reference(a, conv_kernel):
    patches = im2col(f64(a))
    mean = np.mean(patches, axis=-1, keepdims=True)
    std = np.std(patches, axis=-1, keepdims=True, ddof=1)
    normed = (patches - mean) / std
    out = mxq(normed, 2, "e4m3") @ mxq(f64(conv_kernel), 0, "e4m3")
    return np.swapaxes(out, 1, 2).reshape(B, O, H, W)

@@ -1,0 +1,205 @@
+import concourse.mybir as mybir
+from concourse.masks import make_identity
+
+F32 = mybir.dt.float32
+BF16 = mybir.dt.bfloat16
+U32 = mybir.dt.uint32
+U8 = mybir.dt.uint8
+FP8X4 = mybir.dt.float8_e4m3fn_x4
+ALU = mybir.AluOpType
+ACT = mybir.ActivationFunctionType
+AX = mybir.AxisListType
+
+P = 128
+PACK = 4
+C = 512
+H = 32
+W = 32
+O = 512
+TAPS = 9
+NPATCH = C * TAPS
+PIX = H * W
+BLK_ROWS = 8
+BLK_PIX = BLK_ROWS * W
+N_BLK = H // BLK_ROWS
+FLOPS = 2 * PIX * NPATCH * O
+
+
+def tile_norm_conv_kernel(tc, a, conv_kernel, out):
+    nc = tc.nc
+    a_v = a.rearrange("b (m t) h w -> m (b t) (h w)", t=PACK)
+    w_v = conv_kernel.rearrange("(m t k) o -> m t (k o)", t=PACK, k=TAPS)
+    out_v = out.rearrange("b (g p) h w -> p (b g) (h w)", p=P)
+
+    with tc.tile_pool(name="keep", bufs=1) as keep, tc.tile_pool(name="wstage", bufs=2) as wstage, tc.tile_pool(
+        name="work", bufs=2
+    ) as work, tc.psum_pool(name="psa", bufs=4) as psa, tc.psum_pool(name="pst", bufs=4) as pst:
+        ident_f = keep.tile([P, P], F32, name="ident_f")
+        make_identity(nc, ident_f[:])
+        ident_b = keep.tile([P, P], BF16, name="ident_b")
+        make_identity(nc, ident_b[:])
+        ones2 = keep.tile([P, 2], BF16, name="ones2")
+        nc.vector.memset(ones2[:], 1.0)
+        warm = keep.tile([P, 1], F32, name="warm")
+        nc.vector.memset(warm[:], 1.0)
+        nc.scalar.activation(out=warm[:], in_=warm[:], func=ACT.Sqrt)
+
+        a_raw = keep.tile([P, PACK, PIX], BF16, name="a_raw")
+        for h in range(2):
+            nc.sync.dma_start(out=a_raw[:, :, h * 512 : (h + 1) * 512], in_=a_v[:, :, h * 512 : (h + 1) * 512])
+        w_raw = []
+        for kh in range(3):
+            wr = keep.tile([P, PACK, 3 * O], BF16, name="w_raw%d" % kh)
+            nc.sync.dma_start(out=wr[:], in_=w_v[:, :, kh * 3 * O : (kh + 1) * 3 * O])
+            w_raw.append(wr)
+
+        eye3 = ident_f[:].rearrange("p (q j) -> p q j", j=W)
+        band = keep.tile([P, 4, W], F32, name="band")
+        nc.vector.tensor_copy(out=band[:], in_=eye3)
+        nc.vector.tensor_add(out=band[:, :, 1:W], in0=band[:, :, 1:W], in1=eye3[:, :, 0 : W - 1])
+        nc.vector.tensor_add(out=band[:, :, 0 : W - 1], in0=band[:, :, 0 : W - 1], in1=eye3[:, :, 1:W])
+        nc.vector.tensor_add(out=band[:, :, 0:1], in0=band[:, :, 0:1], in1=eye3[:, :, 1:2])
+        nc.vector.tensor_add(out=band[:, :, W - 1 : W], in0=band[:, :, W - 1 : W], in1=eye3[:, :, W - 2 : W - 1])
+        spread = keep.tile([P, 4, W, PACK], F32, name="spread")
+        nc.vector.tensor_copy(out=spread[:], in_=band[:].unsqueeze(3).to_broadcast([P, 4, W, PACK]))
+
+        gram = [psa.tile([P, 4, P], F32, name="gram%d" % h, tag="acc") for h in range(2)]
+        s1p = psa.tile([P, 8, 2], F32, name="s1p", tag="acc")
+        for b in range(8):
+            for t in range(PACK):
+                blk = a_raw[:, t, b * P : (b + 1) * P]
+                nc.tensor.matmul(out=gram[b // 4][:, b % 4, :], lhsT=blk, rhs=blk, start=(t == 0), stop=(t == PACK - 1))
+            for t in range(PACK):
+                blk = a_raw[:, t, b * P : (b + 1) * P]
+                nc.tensor.matmul(out=s1p[:, b, :], lhsT=blk, rhs=ones2[:], start=(t == 0), stop=(t == PACK - 1))
+
+        a_gp = keep.tile([P, H, W + 2, PACK], BF16, name="a_gp")
+        a_rjt = a_raw[:].rearrange("p t (r j) -> p r j t", j=W)
+        for h in range(2):
+            rows = slice(h * 16, (h + 1) * 16)
+            nc.vector.tensor_copy(out=a_gp[:, rows, 1 : W + 1, :], in_=a_rjt[:, rows, :, :])
+        nc.vector.tensor_copy(out=a_gp[:, :, 0 : W + 2 : W + 1, :], in_=a_gp[:, :, 2 : W : W - 3, :])
+
+        sums = keep.tile([P, 2, 8], F32, name="sums")
+        diag = keep.tile([P, 8, P], F32, name="diag")
+        nc.vector.tensor_copy(out=sums[:, 0, :], in_=s1p[:, :, 0])
+        for h in range(2):
+            nc.vector.tensor_tensor(
+                out=diag[:, h * 4 : (h + 1) * 4, :],
+                in0=gram[h][:],
+                in1=ident_f[:].unsqueeze(1).to_broadcast([P, 4, P]),
+                op=ALU.mult,
+            )
+        nc.vector.tensor_reduce(out=sums[:, 1, :], in_=diag[:], axis=AX.X, op=ALU.add)
+        hsum = psa.tile([P, 4, 16], F32, name="hsum", tag="acc")
+        for q in range(4):
+            nc.tensor.matmul(
+                out=hsum[:, q, :],
+                lhsT=spread[:, q, :, :].rearrange("p j t -> p (j t)"),
+                rhs=sums[:].rearrange("p s b -> p (s b)"),
+                start=True,
+                stop=True,
+            )
+        hpad = keep.tile([P, 2, H + 2], F32, name="hpad")
+        nc.vector.tensor_copy(
+            out=hpad[:, :, 1 : H + 1].rearrange("p s (b q) -> p s b q", q=4),
+            in_=hsum[:].rearrange("p q (s b) -> p s b q", s=2),
+        )
+        nc.vector.tensor_copy(out=hpad[:, :, 0 : H + 2 : H + 1], in_=hpad[:, :, 2 : H : H - 3])
+        box = keep.tile([P, 2, H], F32, name="box")
+        nc.vector.tensor_add(out=box[:], in0=hpad[:, :, 0:H], in1=hpad[:, :, 1 : H + 1])
+        nc.vector.tensor_add(out=box[:], in0=box[:], in1=hpad[:, :, 2 : H + 2])
+        mean = keep.tile([P, H], F32, name="mean")
+        nc.vector.tensor_scalar_mul(out=mean[:], in0=box[:, 0, :], scalar1=1.0 / NPATCH)
+        dev = keep.tile([P, H], F32, name="dev")
+        nc.vector.tensor_mul(out=dev[:], in0=mean[:], in1=box[:, 0, :])
+        nc.vector.tensor_sub(out=dev[:], in0=box[:, 1, :], in1=dev[:])
+        std = keep.tile([P, H], F32, name="std")
+        nc.scalar.activation(out=std[:], in_=dev[:], func=ACT.Sqrt, scale=1.0 / (NPATCH - 1))
+        rstd = keep.tile([P, H], F32, name="rstd")
+        nc.vector.reciprocal(out=rstd[:], in_=std[:])
+
+        n_fwd = (H + 2) * 3
+        a_t = keep.tile([P, n_fwd * P], BF16, name="a_t")
+        for g in range(0, n_fwd, 8):
+            cnt = min(8, n_fwd - g)
+            pt = pst.tile([P, 8 * P], BF16, name="pt", tag="tp")
+            for u in range(cnt):
+                prow, kw = divmod(g + u, 3)
+                row = 1 if prow == 0 else (H - 2 if prow == H + 1 else prow - 1)
+                nc.tensor.transpose(
+                    pt[:, u * P : (u + 1) * P],
+                    a_gp[:, row, kw : kw + W, :].rearrange("p j t -> p (j t)"),
+                    ident_b[:],
+                )
+            if (g // 8) % 2 == 0:
+                nc.scalar.copy(out=a_t[:, g * P : (g + cnt) * P], in_=pt[:, 0 : cnt * P])
+            else:
+                nc.vector.tensor_copy(out=a_t[:, g * P : (g + cnt) * P], in_=pt[:, 0 : cnt * P])
+
+        w_codes = keep.tile([P, TAPS, O], U32, name="w_codes", align_bytes=64)
+        w_scales = keep.tile([P, TAPS, O], U8, name="w_scales", align_bytes=64)
+        for t0 in range(0, TAPS, 2):
+            cnt = min(2, TAPS - t0)
+            wg = wstage.tile([P, 2, O * PACK], BF16, name="wg", align_bytes=64)
+            for u in range(cnt):
+                kh, kw = divmod(t0 + u, 3)
+                src = w_raw[kh][:, :, kw * O : (kw + 1) * O]
+                dst = wg[:, u, :].rearrange("p (o t) -> p o t", t=PACK)
+                if u == 1 and t0 % 4 == 0:
+                    nc.scalar.copy(out=dst, in_=src.rearrange("p t o -> p o t"))
+                else:
+                    nc.vector.tensor_copy(
+                        out=dst.rearrange("p (c i) t -> p c t i", i=4), in_=src.rearrange("p t (c i) -> p c t i", i=4)
+                    )
+            nc.vector.quantize_mx(
+                out=w_codes[:, t0 : t0 + cnt, :].rearrange("p a b -> p (a b)").bitcast(FP8X4),
+                scales=w_scales[:, t0 : t0 + cnt, :].rearrange("p a b -> p (a b)"),
+                in_=wg[:, 0:cnt, :].rearrange("p a b -> p (a b)"),
+            )
+
+        for blk in range(N_BLK):
+            nrm = work.tile([P, BLK_ROWS, TAPS * P], BF16, name="nrm")
+            for rr in range(BLK_ROWS):
+                r = blk * BLK_ROWS + rr
+                nc.vector.tensor_scalar(
+                    out=nrm[:, rr, :],
+                    in0=a_t[:, r * 3 * P : (r * 3 + TAPS) * P],
+                    scalar1=mean[:, r : r + 1],
+                    scalar2=rstd[:, r : r + 1],
+                    op0=ALU.subtract,
+                    op1=ALU.mult,
+                )
+            grp = work.tile([P, TAPS, BLK_PIX * PACK], BF16, name="grp", align_bytes=64)
+            codes = work.tile([P, TAPS, BLK_PIX], U32, name="codes", align_bytes=64)
+            scales = work.tile([P, TAPS, BLK_PIX], U8, name="scales", align_bytes=64)
+            for tap in range(TAPS):
+                pb = pst.tile([P, 8 * P], BF16, name="pb", tag="tp")
+                for rr in range(BLK_ROWS):
+                    nc.tensor.transpose(pb[:, rr * P : (rr + 1) * P], nrm[:, rr, tap * P : (tap + 1) * P], ident_b[:])
+                nc.scalar.copy(out=grp[:, tap, :], in_=pb[:])
+            for t0, t1 in ((0, 4), (4, 8), (8, 9)):
+                nc.vector.quantize_mx(
+                    out=codes[:, t0:t1, :].rearrange("p a b -> p (a b)").bitcast(FP8X4),
+                    scales=scales[:, t0:t1, :].rearrange("p a b -> p (a b)"),
+                    in_=grp[:, t0:t1, :].rearrange("p a b -> p (a b)"),
+                )
+            for half in range(2):
+                acc = psa.tile([P, 2, BLK_PIX], F32, name="acc", tag="acc")
+                for oo in range(2):
+                    ot = half * 2 + oo
+                    for tap in range(TAPS):
+                        nc.tensor.matmul_mx(
+                            out=acc[:, oo, :],
+                            lhsT=w_codes[:, tap, ot * P : (ot + 1) * P].bitcast(FP8X4),
+                            lhsT_scale=w_scales[:, tap, ot * P : (ot + 1) * P],
+                            rhs=codes[:, tap, :].bitcast(FP8X4),
+                            rhs_scale=scales[:, tap, :],
+                            start=(tap == 0),
+                            stop=(tap == TAPS - 1),
+                        )
+                res = work.tile([P, 2, BLK_PIX], F32, name="res")
+                nc.vector.tensor_copy(out=res[:], in_=acc[:])
+                nc.sync.dma_start(
+                    out=out_v[:, half * 2 : half * 2 + 2, blk * BLK_PIX : (blk + 1) * BLK_PIX], in_=res[:]
+                )

@@ -21,7 +21,9 @@ NPATCH = C * TAPS
 PIX = H * W
 BLK_ROWS = 8
 BLK_PIX = BLK_ROWS * W
-N_BLK = H // BLK_ROWS
+N_UNITS = 12
+LAG = 3
+ROWS_A = 20
 FLOPS = 2 * PIX * NPATCH * O
 
 
@@ -31,9 +33,11 @@ def tile_norm_conv_kernel(tc, a, conv_kernel, out):
     w_v = conv_kernel.rearrange("(m t k) o -> m t (k o)", t=PACK, k=TAPS)
     out_v = out.rearrange("b (g p) h w -> p (b g) (h w)", p=P)
 
-    with tc.tile_pool(name="keep", bufs=1) as keep, tc.tile_pool(name="wstage", bufs=2) as wstage, tc.tile_pool(
-        name="work", bufs=2
-    ) as work, tc.psum_pool(name="psa", bufs=4) as psa, tc.psum_pool(name="pst", bufs=4) as pst:
+    with tc.tile_pool(name="keep", bufs=1) as keep, tc.tile_pool(name="nrmp", bufs=2) as nrmp, tc.tile_pool(
+        name="grpp", bufs=4
+    ) as grpp, tc.tile_pool(name="codep", bufs=5) as codep, tc.tile_pool(name="resp", bufs=4) as resp, tc.psum_pool(
+        name="psum", bufs=1
+    ) as psum, tc.manual_schedule():
         ident_f = keep.tile([P, P], F32, name="ident_f")
         make_identity(nc, ident_f[:])
         ident_b = keep.tile([P, P], BF16, name="ident_b")
@@ -44,9 +48,10 @@ def tile_norm_conv_kernel(tc, a, conv_kernel, out):
         nc.vector.memset(warm[:], 1.0)
         nc.scalar.activation(out=warm[:], in_=warm[:], func=ACT.Sqrt)
 
+        pix_a = ROWS_A * W
         a_raw = keep.tile([P, PACK, PIX], BF16, name="a_raw")
-        for h in range(2):
-            nc.sync.dma_start(out=a_raw[:, :, h * 512 : (h + 1) * 512], in_=a_v[:, :, h * 512 : (h + 1) * 512])
+        nc.sync.dma_start(out=a_raw[:, :, 0:pix_a], in_=a_v[:, :, 0:pix_a])
+        nc.sync.dma_start(out=a_raw[:, :, pix_a:PIX], in_=a_v[:, :, pix_a:PIX])
         w_raw = []
         for kh in range(3):
             wr = keep.tile([P, PACK, 3 * O], BF16, name="w_raw%d" % kh)
@@ -63,143 +68,253 @@ def tile_norm_conv_kernel(tc, a, conv_kernel, out):
         spread = keep.tile([P, 4, W, PACK], F32, name="spread")
         nc.vector.tensor_copy(out=spread[:], in_=band[:].unsqueeze(3).to_broadcast([P, 4, W, PACK]))
 
-        gram = [psa.tile([P, 4, P], F32, name="gram%d" % h, tag="acc") for h in range(2)]
-        s1p = psa.tile([P, 8, 2], F32, name="s1p", tag="acc")
-        for b in range(8):
-            for t in range(PACK):
-                blk = a_raw[:, t, b * P : (b + 1) * P]
-                nc.tensor.matmul(out=gram[b // 4][:, b % 4, :], lhsT=blk, rhs=blk, start=(t == 0), stop=(t == PACK - 1))
-            for t in range(PACK):
-                blk = a_raw[:, t, b * P : (b + 1) * P]
-                nc.tensor.matmul(out=s1p[:, b, :], lhsT=blk, rhs=ones2[:], start=(t == 0), stop=(t == PACK - 1))
-
         a_gp = keep.tile([P, H, W + 2, PACK], BF16, name="a_gp")
         a_rjt = a_raw[:].rearrange("p t (r j) -> p r j t", j=W)
-        for h in range(2):
-            rows = slice(h * 16, (h + 1) * 16)
-            nc.vector.tensor_copy(out=a_gp[:, rows, 1 : W + 1, :], in_=a_rjt[:, rows, :, :])
-        nc.vector.tensor_copy(out=a_gp[:, :, 0 : W + 2 : W + 1, :], in_=a_gp[:, :, 2 : W : W - 3, :])
-
-        sums = keep.tile([P, 2, 8], F32, name="sums")
-        diag = keep.tile([P, 8, P], F32, name="diag")
-        nc.vector.tensor_copy(out=sums[:, 0, :], in_=s1p[:, :, 0])
-        for h in range(2):
-            nc.vector.tensor_tensor(
-                out=diag[:, h * 4 : (h + 1) * 4, :],
-                in0=gram[h][:],
-                in1=ident_f[:].unsqueeze(1).to_broadcast([P, 4, P]),
-                op=ALU.mult,
-            )
-        nc.vector.tensor_reduce(out=sums[:, 1, :], in_=diag[:], axis=AX.X, op=ALU.add)
-        hsum = psa.tile([P, 4, 16], F32, name="hsum", tag="acc")
-        for q in range(4):
-            nc.tensor.matmul(
-                out=hsum[:, q, :],
-                lhsT=spread[:, q, :, :].rearrange("p j t -> p (j t)"),
-                rhs=sums[:].rearrange("p s b -> p (s b)"),
-                start=True,
-                stop=True,
-            )
-        hpad = keep.tile([P, 2, H + 2], F32, name="hpad")
-        nc.vector.tensor_copy(
-            out=hpad[:, :, 1 : H + 1].rearrange("p s (b q) -> p s b q", q=4),
-            in_=hsum[:].rearrange("p q (s b) -> p s b q", s=2),
-        )
-        nc.vector.tensor_copy(out=hpad[:, :, 0 : H + 2 : H + 1], in_=hpad[:, :, 2 : H : H - 3])
-        box = keep.tile([P, 2, H], F32, name="box")
-        nc.vector.tensor_add(out=box[:], in0=hpad[:, :, 0:H], in1=hpad[:, :, 1 : H + 1])
-        nc.vector.tensor_add(out=box[:], in0=box[:], in1=hpad[:, :, 2 : H + 2])
-        mean = keep.tile([P, H], F32, name="mean")
-        nc.vector.tensor_scalar_mul(out=mean[:], in0=box[:, 0, :], scalar1=1.0 / NPATCH)
-        dev = keep.tile([P, H], F32, name="dev")
-        nc.vector.tensor_mul(out=dev[:], in0=mean[:], in1=box[:, 0, :])
-        nc.vector.tensor_sub(out=dev[:], in0=box[:, 1, :], in1=dev[:])
-        std = keep.tile([P, H], F32, name="std")
-        nc.scalar.activation(out=std[:], in_=dev[:], func=ACT.Sqrt, scale=1.0 / (NPATCH - 1))
-        rstd = keep.tile([P, H], F32, name="rstd")
-        nc.vector.reciprocal(out=rstd[:], in_=std[:])
-
         n_fwd = (H + 2) * 3
         a_t = keep.tile([P, n_fwd * P], BF16, name="a_t")
-        for g in range(0, n_fwd, 8):
-            cnt = min(8, n_fwd - g)
-            pt = pst.tile([P, 8 * P], BF16, name="pt", tag="tp")
-            for u in range(cnt):
-                prow, kw = divmod(g + u, 3)
-                row = 1 if prow == 0 else (H - 2 if prow == H + 1 else prow - 1)
-                nc.tensor.transpose(
-                    pt[:, u * P : (u + 1) * P],
-                    a_gp[:, row, kw : kw + W, :].rearrange("p j t -> p (j t)"),
-                    ident_b[:],
-                )
-            if (g // 8) % 2 == 0:
-                nc.scalar.copy(out=a_t[:, g * P : (g + cnt) * P], in_=pt[:, 0 : cnt * P])
-            else:
-                nc.vector.tensor_copy(out=a_t[:, g * P : (g + cnt) * P], in_=pt[:, 0 : cnt * P])
-
+        sums = keep.tile([P, 8, 2], F32, name="sums")
+        diag = keep.tile([P, 5, P], F32, name="diag")
+        hpad = keep.tile([P, 2, H + 2], F32, name="hpad")
+        box = keep.tile([P, 2, H], F32, name="box")
+        mean = keep.tile([P, H], F32, name="mean")
+        dev = keep.tile([P, H], F32, name="dev")
+        std = keep.tile([P, H], F32, name="std")
+        rstd = keep.tile([P, H], F32, name="rstd")
         w_codes = keep.tile([P, TAPS, O], U32, name="w_codes", align_bytes=64)
         w_scales = keep.tile([P, TAPS, O], U8, name="w_scales", align_bytes=64)
-        for t0 in range(0, TAPS, 2):
-            cnt = min(2, TAPS - t0)
-            wg = wstage.tile([P, 2, O * PACK], BF16, name="wg", align_bytes=64)
-            for u in range(cnt):
-                kh, kw = divmod(t0 + u, 3)
-                src = w_raw[kh][:, :, kw * O : (kw + 1) * O]
-                dst = wg[:, u, :].rearrange("p (o t) -> p o t", t=PACK)
-                if u == 1 and t0 % 4 == 0:
-                    nc.scalar.copy(out=dst, in_=src.rearrange("p t o -> p o t"))
-                else:
-                    nc.vector.tensor_copy(
-                        out=dst.rearrange("p (c i) t -> p c t i", i=4), in_=src.rearrange("p t (c i) -> p c t i", i=4)
+        wg = [keep.tile([P, O * PACK], BF16, name="wg%d" % tap, align_bytes=64) for tap in range(TAPS)]
+
+        gram = [psum.tile([P, 4, P], F32, name="gram%d" % h, tag="bk%d" % h) for h in range(2)]
+        s1p = psum.tile([P, 8, 2], F32, name="s1p", tag="bk2")
+        hs = psum.tile([P, 4, 8, 2], F32, name="hs", tag="bk3")
+        state = {"tp": 0}
+
+        def tp_bank(name):
+            bank = 4 + state["tp"] % 4
+            state["tp"] = state["tp"] + 1
+            return psum.tile([P, 8 * P], BF16, name=name, tag="bk%d" % bank)
+
+        def gram_blocks(b0, b1):
+            for b in range(b0, b1):
+                for t in range(PACK):
+                    blk = a_raw[:, t, b * P : (b + 1) * P]
+                    nc.tensor.matmul(
+                        out=gram[b // 4][:, b % 4, :], lhsT=blk, rhs=blk, start=(t == 0), stop=(t == PACK - 1)
                     )
-            nc.vector.quantize_mx(
-                out=w_codes[:, t0 : t0 + cnt, :].rearrange("p a b -> p (a b)").bitcast(FP8X4),
-                scales=w_scales[:, t0 : t0 + cnt, :].rearrange("p a b -> p (a b)"),
-                in_=wg[:, 0:cnt, :].rearrange("p a b -> p (a b)"),
+            for b in range(b0, b1):
+                for t in range(PACK):
+                    blk = a_raw[:, t, b * P : (b + 1) * P]
+                    nc.tensor.matmul(out=s1p[:, b, :], lhsT=blk, rhs=ones2[:], start=(t == 0), stop=(t == PACK - 1))
+
+        def regroup_a(r0, r1):
+            nc.vector.tensor_copy(out=a_gp[:, r0:r1, 1 : W + 1, :], in_=a_rjt[:, r0:r1, :, :])
+            nc.vector.tensor_copy(out=a_gp[:, r0:r1, 0 : W + 2 : W + 1, :], in_=a_gp[:, r0:r1, 2 : W : W - 3, :])
+
+        def square_sums(b0, b1):
+            for h in range(2):
+                lo = max(b0, 4 * h)
+                hi = min(b1, 4 * h + 4)
+                if lo < hi:
+                    nc.vector.tensor_tensor(
+                        out=diag[:, lo - b0 : hi - b0, :],
+                        in0=gram[h][:, lo - 4 * h : hi - 4 * h, :],
+                        in1=ident_f[:].unsqueeze(1).to_broadcast([P, hi - lo, P]),
+                        op=ALU.mult,
+                    )
+            nc.vector.tensor_reduce(out=sums[:, b0:b1, 1], in_=diag[:, 0 : b1 - b0, :], axis=AX.X, op=ALU.add)
+
+        def plain_sums(b0, b1):
+            nc.vector.tensor_copy(out=sums[:, b0:b1, 0], in_=s1p[:, b0:b1, 0])
+
+        def row_sums(b0, b1):
+            for q in range(4):
+                nc.tensor.matmul(
+                    out=hs[:, q, b0:b1, :].rearrange("p b s -> p (b s)"),
+                    lhsT=spread[:, q, :, :].rearrange("p j t -> p (j t)"),
+                    rhs=sums[:, b0:b1, :].rearrange("p b s -> p (b s)"),
+                    start=True,
+                    stop=True,
+                )
+
+        def fetch_row_sums(b0, b1):
+            nc.vector.tensor_copy(
+                out=hpad[:, :, 1 + 4 * b0 : 1 + 4 * b1].rearrange("p s (b q) -> p s b q", q=4),
+                in_=hs[:, :, b0:b1, :].rearrange("p q b s -> p s b q"),
             )
 
-        for blk in range(N_BLK):
-            nrm = work.tile([P, BLK_ROWS, TAPS * P], BF16, name="nrm")
+        def variance(r0, r1, pad_to, pad_from):
+            nc.vector.tensor_copy(out=hpad[:, :, pad_to : pad_to + 1], in_=hpad[:, :, pad_from : pad_from + 1])
+            nc.vector.tensor_add(out=box[:, :, r0:r1], in0=hpad[:, :, r0:r1], in1=hpad[:, :, r0 + 1 : r1 + 1])
+            nc.vector.tensor_add(out=box[:, :, r0:r1], in0=box[:, :, r0:r1], in1=hpad[:, :, r0 + 2 : r1 + 2])
+            nc.vector.scalar_tensor_tensor(
+                out=dev[:, r0:r1],
+                in0=box[:, 0, r0:r1],
+                scalar=1.0 / NPATCH,
+                in1=box[:, 0, r0:r1],
+                op0=ALU.mult,
+                op1=ALU.mult,
+            )
+            nc.vector.tensor_sub(out=dev[:, r0:r1], in0=box[:, 1, r0:r1], in1=dev[:, r0:r1])
+            nc.scalar.activation(out=std[:, r0:r1], in_=dev[:, r0:r1], func=ACT.Sqrt, scale=1.0 / (NPATCH - 1))
+            nc.vector.tensor_scalar_mul(out=mean[:, r0:r1], in0=box[:, 0, r0:r1], scalar1=1.0 / NPATCH)
+
+        def inverse_std(r0, r1):
+            nc.vector.reciprocal(out=rstd[:, r0:r1], in_=std[:, r0:r1])
+
+        def forward(g0, g1):
+            for g in range(g0, g1):
+                first = g * 8
+                cnt = min(8, n_fwd - first)
+                pt = tp_bank("pt")
+                for u in range(cnt):
+                    prow, kw = divmod(first + u, 3)
+                    row = 1 if prow == 0 else (H - 2 if prow == H + 1 else prow - 1)
+                    nc.tensor.transpose(
+                        pt[:, u * P : (u + 1) * P],
+                        a_gp[:, row, kw : kw + W, :].rearrange("p j t -> p (j t)"),
+                        ident_b[:],
+                    )
+                nc.scalar.copy(out=a_t[:, first * P : (first + cnt) * P], in_=pt[:, 0 : cnt * P])
+
+        def regroup_w(eng, tap, o0, o1):
+            kh, kw = divmod(tap, 3)
+            src = w_raw[kh][:, :, kw * O + o0 : kw * O + o1].rearrange("p t (c i) -> p c t i", i=4)
+            dst = wg[tap][:, o0 * PACK : o1 * PACK].rearrange("p (c i t) -> p c t i", i=4, t=PACK)
+            if eng == "v":
+                nc.vector.tensor_copy(out=dst, in_=src)
+            else:
+                nc.scalar.copy(out=dst, in_=src)
+
+        def quantise_w(tap):
+            nc.vector.quantize_mx(
+                out=w_codes[:, tap, :].bitcast(FP8X4), scales=w_scales[:, tap, :], in_=wg[tap][:]
+            )
+
+        nrm = {}
+
+        def normalise(blk):
+            nrm[blk] = nrmp.tile([P, BLK_ROWS, TAPS * P], BF16, name="nrm")
             for rr in range(BLK_ROWS):
                 r = blk * BLK_ROWS + rr
                 nc.vector.tensor_scalar(
-                    out=nrm[:, rr, :],
+                    out=nrm[blk][:, rr, :],
                     in0=a_t[:, r * 3 * P : (r * 3 + TAPS) * P],
                     scalar1=mean[:, r : r + 1],
                     scalar2=rstd[:, r : r + 1],
                     op0=ALU.subtract,
                     op1=ALU.mult,
                 )
-            grp = work.tile([P, TAPS, BLK_PIX * PACK], BF16, name="grp", align_bytes=64)
-            codes = work.tile([P, TAPS, BLK_PIX], U32, name="codes", align_bytes=64)
-            scales = work.tile([P, TAPS, BLK_PIX], U8, name="scales", align_bytes=64)
-            for tap in range(TAPS):
-                pb = pst.tile([P, 8 * P], BF16, name="pb", tag="tp")
-                for rr in range(BLK_ROWS):
-                    nc.tensor.transpose(pb[:, rr * P : (rr + 1) * P], nrm[:, rr, tap * P : (tap + 1) * P], ident_b[:])
-                nc.scalar.copy(out=grp[:, tap, :], in_=pb[:])
-            for t0, t1 in ((0, 4), (4, 8), (8, 9)):
+
+        grp = {}
+        codes = {}
+        scales = {}
+
+        def backward(unit, by_rows):
+            blk, kh = divmod(unit, 3)
+            banks = [tp_bank("pb%d" % i) for i in range(3)]
+            order = [(rr, i) for rr in range(BLK_ROWS) for i in range(3)]
+            if not by_rows:
+                order = [(rr, i) for i in range(3) for rr in range(BLK_ROWS)]
+            for rr, i in order:
+                tap = kh * 3 + i
+                nc.tensor.transpose(
+                    banks[i][:, rr * P : (rr + 1) * P], nrm[blk][:, rr, tap * P : (tap + 1) * P], ident_b[:]
+                )
+            grp[unit] = grpp.tile([P, 3, BLK_PIX * PACK], BF16, name="grp", align_bytes=64)
+            for i in range(3):
+                nc.scalar.copy(out=grp[unit][:, i, :], in_=banks[i][:])
+
+        def quantise(unit):
+            codes[unit] = codep.tile([P, 3, BLK_PIX], U32, name="codes", align_bytes=64)
+            scales[unit] = codep.tile([P, 3, BLK_PIX], U8, name="scales", align_bytes=64)
+            for t0, t1 in ((0, 2), (2, 3)):
                 nc.vector.quantize_mx(
-                    out=codes[:, t0:t1, :].rearrange("p a b -> p (a b)").bitcast(FP8X4),
-                    scales=scales[:, t0:t1, :].rearrange("p a b -> p (a b)"),
-                    in_=grp[:, t0:t1, :].rearrange("p a b -> p (a b)"),
+                    out=codes[unit][:, t0:t1, :].rearrange("p a b -> p (a b)").bitcast(FP8X4),
+                    scales=scales[unit][:, t0:t1, :].rearrange("p a b -> p (a b)"),
+                    in_=grp[unit][:, t0:t1, :].rearrange("p a b -> p (a b)"),
                 )
-            for half in range(2):
-                acc = psa.tile([P, 2, BLK_PIX], F32, name="acc", tag="acc")
-                for oo in range(2):
-                    ot = half * 2 + oo
-                    for tap in range(TAPS):
-                        nc.tensor.matmul_mx(
-                            out=acc[:, oo, :],
-                            lhsT=w_codes[:, tap, ot * P : (ot + 1) * P].bitcast(FP8X4),
-                            lhsT_scale=w_scales[:, tap, ot * P : (ot + 1) * P],
-                            rhs=codes[:, tap, :].bitcast(FP8X4),
-                            rhs_scale=scales[:, tap, :],
-                            start=(tap == 0),
-                            stop=(tap == TAPS - 1),
-                        )
-                res = work.tile([P, 2, BLK_PIX], F32, name="res")
-                nc.vector.tensor_copy(out=res[:], in_=acc[:])
-                nc.sync.dma_start(
-                    out=out_v[:, half * 2 : half * 2 + 2, blk * BLK_PIX : (blk + 1) * BLK_PIX], in_=res[:]
-                )
+
+        acc = {}
+
+        def multiply(unit):
+            blk, kh = divmod(unit, 3)
+            for ot in range(4):
+                if kh == 0:
+                    acc[ot] = psum.tile([P, BLK_PIX], F32, name="acc%d" % ot, tag="bk%d" % ot)
+                for i in range(3):
+                    tap = kh * 3 + i
+                    nc.tensor.matmul_mx(
+                        out=acc[ot][:],
+                        lhsT=w_codes[:, tap, ot * P : (ot + 1) * P].bitcast(FP8X4),
+                        lhsT_scale=w_scales[:, tap, ot * P : (ot + 1) * P],
+                        rhs=codes[unit][:, i, :].bitcast(FP8X4),
+                        rhs_scale=scales[unit][:, i, :],
+                        start=(tap == 0),
+                        stop=(tap == TAPS - 1),
+                    )
+                if kh == 2:
+                    res = resp.tile([P, BLK_PIX], F32, name="res")
+                    nc.scalar.copy(out=res[:], in_=acc[ot][:])
+                    nc.sync.dma_start(out=out_v[:, ot, blk * BLK_PIX : (blk + 1) * BLK_PIX], in_=res[:])
+
+        gram_blocks(0, 5)
+        regroup_a(0, ROWS_A)
+        regroup_a(ROWS_A, H)
+        square_sums(0, 5)
+        plain_sums(0, 5)
+        regroup_w("s", 2, 0, O // 2)
+        forward(0, 4)
+        row_sums(0, 5)
+        regroup_w("v", 0, 0, O)
+        regroup_w("v", 1, 0, O)
+        quantise_w(0)
+        quantise_w(1)
+        regroup_w("s", 2, O // 2, O)
+        fetch_row_sums(0, 5)
+        variance(0, 16, 0, 2)
+        gram_blocks(5, 8)
+        square_sums(5, 8)
+        inverse_std(0, 16)
+        regroup_w("s", 5, 0, O // 2)
+        forward(4, 7)
+        normalise(0)
+        regroup_w("s", 5, O // 2, O)
+        regroup_w("s", 7, 0, O // 2)
+        backward(0, True)
+        plain_sums(5, 8)
+        quantise_w(2)
+        normalise(1)
+        backward(1, False)
+        backward(2, False)
+        row_sums(5, 8)
+        quantise(0)
+        regroup_w("v", 3, 0, O)
+        regroup_w("v", 4, 0, O)
+        fetch_row_sums(5, 8)
+        quantise(1)
+        quantise_w(3)
+        quantise_w(4)
+        quantise_w(5)
+        regroup_w("v", 6, 0, O)
+        quantise(2)
+        regroup_w("s", 7, O // 2, O)
+        forward(7, 10)
+        regroup_w("s", 8, 0, O // 2)
+        regroup_w("s", 8, O // 2, O)
+        quantise_w(6)
+        quantise_w(7)
+        quantise_w(8)
+
+        for slot in range(LAG, N_UNITS + LAG):
+            if slot == 6:
+                forward(10, 13)
+                normalise(3)
+            multiply(slot - LAG)
+            if slot < N_UNITS:
+                backward(slot, False)
+                if slot == 4:
+                    variance(16, H, H + 1, H - 1)
+                quantise(slot)
+            if slot == 4:
+                inverse_std(16, H)
+                normalise(2)

@@ -174,7 +174,7 @@ def tile_norm_conv_kernel(tc, a, conv_kernel, out):
                         a_gp[:, row, kw : kw + W, :].rearrange("p j t -> p (j t)"),
                         ident_b[:],
                     )
-                nc.scalar.copy(out=a_t[:, first * P : (first + cnt) * P], in_=pt[:, 0 : cnt * P])
+                nc.scalar.copy(out=a_t[:, first * P : (first + cnt) * P].bitcast(F32), in_=pt[:, 0 : cnt * P].bitcast(F32))
 
         def regroup_w(eng, tap, o0, o1):
             kh, kw = divmod(tap, 3)
@@ -222,7 +222,7 @@ def tile_norm_conv_kernel(tc, a, conv_kernel, out):
                 )
             grp[unit] = grpp.tile([P, 3, BLK_PIX * PACK], BF16, name="grp", align_bytes=64)
             for i in range(3):
-                nc.scalar.copy(out=grp[unit][:, i, :], in_=banks[i][:])
+                nc.scalar.copy(out=grp[unit][:, i, :].bitcast(F32), in_=banks[i][:].bitcast(F32))
 
         def quantise(unit):
             codes[unit] = codep.tile([P, 3, BLK_PIX], U32, name="codes", align_bytes=64)

@@ -38,10 +38,12 @@ def tile_norm_conv_kernel(tc, a, conv_kernel, out):
     ) as grpp, tc.tile_pool(name="codep", bufs=5) as codep, tc.tile_pool(name="resp", bufs=4) as resp, tc.psum_pool(
         name="psum", bufs=1
     ) as psum, tc.manual_schedule():
-        ident_f = keep.tile([P, P], F32, name="ident_f")
-        make_identity(nc, ident_f[:])
+        filler = keep.tile([P, 512], BF16, name="filler")
+        nc.vector.memset(filler[:], 0.0)
         ident_b = keep.tile([P, P], BF16, name="ident_b")
         make_identity(nc, ident_b[:])
+        ident_f = keep.tile([P, P], F32, name="ident_f")
+        make_identity(nc, ident_f[:])
         ones2 = keep.tile([P, 2], BF16, name="ones2")
         nc.vector.memset(ones2[:], 1.0)
         warm = keep.tile([P, 1], F32, name="warm")
@@ -87,7 +89,17 @@ def tile_norm_conv_kernel(tc, a, conv_kernel, out):
         gram = [psum.tile([P, 4, P], F32, name="gram%d" % h, tag="bk%d" % h) for h in range(2)]
         s1p = psum.tile([P, 8, 2], F32, name="s1p", tag="bk2")
         hs = psum.tile([P, 4, 8, 2], F32, name="hs", tag="bk3")
-        state = {"tp": 0}
+        state = {"tp": 0, "since": 0, "spare": None}
+
+        def keep_clock():
+            nc.tensor.matmul(out=state["spare"][:], lhsT=ident_b[:], rhs=filler[:], start=True, stop=True)
+
+        def count_transpose():
+            if state["spare"] is not None:
+                state["since"] = state["since"] + 1
+                if state["since"] == 12:
+                    state["since"] = 0
+                    keep_clock()
 
         def tp_bank(name):
             bank = 4 + state["tp"] % 4
@@ -174,6 +186,7 @@ def tile_norm_conv_kernel(tc, a, conv_kernel, out):
                         a_gp[:, row, kw : kw + W, :].rearrange("p j t -> p (j t)"),
                         ident_b[:],
                     )
+                    count_transpose()
                 nc.scalar.copy(out=a_t[:, first * P : (first + cnt) * P].bitcast(F32), in_=pt[:, 0 : cnt * P].bitcast(F32))
 
         def regroup_w(eng, tap, o0, o1):
@@ -220,6 +233,7 @@ def tile_norm_conv_kernel(tc, a, conv_kernel, out):
                 nc.tensor.transpose(
                     banks[i][:, rr * P : (rr + 1) * P], nrm[blk][:, rr, tap * P : (tap + 1) * P], ident_b[:]
                 )
+                count_transpose()
             grp[unit] = grpp.tile([P, 3, BLK_PIX * PACK], BF16, name="grp", align_bytes=64)
             for i in range(3):
                 nc.scalar.copy(out=grp[unit][:, i, :].bitcast(F32), in_=banks[i][:].bitcast(F32))
@@ -257,11 +271,15 @@ def tile_norm_conv_kernel(tc, a, conv_kernel, out):
                     nc.scalar.copy(out=res[:], in_=acc[ot][:])
                     nc.sync.dma_start(out=out_v[:, ot, blk * BLK_PIX : (blk + 1) * BLK_PIX], in_=res[:])
 
+        state["spare"] = psum.tile([P, 512], F32, name="spare_a", tag="bk7")
+        for i in range(3):
+            keep_clock()
         gram_blocks(0, 5)
         regroup_a(0, ROWS_A)
         regroup_a(ROWS_A, H)
         square_sums(0, 5)
         plain_sums(0, 5)
+        state["spare"] = psum.tile([P, 512], F32, name="spare_b", tag="bk0")
         regroup_w("s", 2, 0, O // 2)
         forward(0, 4)
         row_sums(0, 5)
@@ -304,6 +322,8 @@ def tile_norm_conv_kernel(tc, a, conv_kernel, out):
         quantise_w(6)
         quantise_w(7)
         quantise_w(8)
+
+        state["spare"] = None
 
         for slot in range(LAG, N_UNITS + LAG):
             if slot == 6:

@@ -19,11 +19,13 @@ O = 512
 TAPS = 9
 NPATCH = C * TAPS
 PIX = H * W
-BLK_ROWS = 8
-BLK_PIX = BLK_ROWS * W
+HALF = H // 2
+BLK_PAIRS = 4
+BLK_PIX = BLK_PAIRS * 2 * W
 N_UNITS = 12
 LAG = 3
-ROWS_A = 20
+TILE = 2 * P
+FILL_EVERY = 8
 FLOPS = 2 * PIX * NPATCH * O
 
 
@@ -31,7 +33,7 @@ def tile_norm_conv_kernel(tc, a, conv_kernel, out):
     nc = tc.nc
     a_v = a.rearrange("b (m t) h w -> m (b t) (h w)", t=PACK)
     w_v = conv_kernel.rearrange("(m t k) o -> m t (k o)", t=PACK, k=TAPS)
-    out_v = out.rearrange("b (g p) h w -> p (b g) (h w)", p=P)
+    out_v = out.rearrange("b (g p) (x r) w -> p (b g) x (r w)", p=P, x=2)
 
     with tc.tile_pool(name="keep", bufs=1) as keep, tc.tile_pool(name="nrmp", bufs=2) as nrmp, tc.tile_pool(
         name="grpp", bufs=4
@@ -50,7 +52,7 @@ def tile_norm_conv_kernel(tc, a, conv_kernel, out):
         nc.vector.memset(warm[:], 1.0)
         nc.scalar.activation(out=warm[:], in_=warm[:], func=ACT.Sqrt)
 
-        pix_a = ROWS_A * W
+        pix_a = (HALF + 1) * W
         a_raw = keep.tile([P, PACK, PIX], BF16, name="a_raw")
         nc.sync.dma_start(out=a_raw[:, :, 0:pix_a], in_=a_v[:, :, 0:pix_a])
         nc.sync.dma_start(out=a_raw[:, :, pix_a:PIX], in_=a_v[:, :, pix_a:PIX])
@@ -69,19 +71,24 @@ def tile_norm_conv_kernel(tc, a, conv_kernel, out):
         nc.vector.tensor_add(out=band[:, :, W - 1 : W], in0=band[:, :, W - 1 : W], in1=eye3[:, :, W - 2 : W - 1])
         spread = keep.tile([P, 4, W, PACK], F32, name="spread")
         nc.vector.tensor_copy(out=spread[:], in_=band[:].unsqueeze(3).to_broadcast([P, 4, W, PACK]))
+        is_x = keep.tile([P, 2], F32, name="is_x")
+        eye_jxu = ident_f[:].rearrange("p (j x u) -> p j x u", x=2, u=2)
+        for x in range(2):
+            nc.vector.tensor_reduce(out=is_x[:, x : x + 1], in_=eye_jxu[:, :, x, :], axis=AX.XY, op=ALU.add)
 
-        a_gp = keep.tile([P, H, W + 2, PACK], BF16, name="a_gp")
+        a_gp = keep.tile([P, HALF + 2, W + 2, 2, PACK], BF16, name="a_gp")
         a_rjt = a_raw[:].rearrange("p t (r j) -> p r j t", j=W)
-        n_fwd = (H + 2) * 3
-        a_t = keep.tile([P, n_fwd * P], BF16, name="a_t")
+        n_fwd = (HALF + 2) * 3
+        a_t = keep.tile([P, n_fwd * TILE], BF16, name="a_t")
         sums = keep.tile([P, 8, 2], F32, name="sums")
-        diag = keep.tile([P, 5, P], F32, name="diag")
+        diag = keep.tile([P, 8, P], F32, name="diag")
         hpad = keep.tile([P, 2, H + 2], F32, name="hpad")
-        box = keep.tile([P, 2, H], F32, name="box")
-        mean = keep.tile([P, H], F32, name="mean")
-        dev = keep.tile([P, H], F32, name="dev")
-        std = keep.tile([P, H], F32, name="std")
-        rstd = keep.tile([P, H], F32, name="rstd")
+        hsel = keep.tile([P, 2, HALF + 2], F32, name="hsel")
+        box = keep.tile([P, 2, HALF], F32, name="box")
+        mean = keep.tile([P, HALF], F32, name="mean")
+        dev = keep.tile([P, HALF], F32, name="dev")
+        std = keep.tile([P, HALF], F32, name="std")
+        rstd = keep.tile([P, HALF], F32, name="rstd")
         w_codes = keep.tile([P, TAPS, O], U32, name="w_codes", align_bytes=64)
         w_scales = keep.tile([P, TAPS, O], U8, name="w_scales", align_bytes=64)
         wg = [keep.tile([P, O * PACK], BF16, name="wg%d" % tap, align_bytes=64) for tap in range(TAPS)]
@@ -91,20 +98,20 @@ def tile_norm_conv_kernel(tc, a, conv_kernel, out):
         hs = psum.tile([P, 4, 8, 2], F32, name="hs", tag="bk3")
         state = {"tp": 0, "since": 0, "spare": None}
 
+        def tp_bank(name):
+            bank = 4 + state["tp"] % 4
+            state["tp"] = state["tp"] + 1
+            return psum.tile([P, 4 * P], F32, name=name, tag="bk%d" % bank)
+
         def keep_clock():
             nc.tensor.matmul(out=state["spare"][:], lhsT=ident_b[:], rhs=filler[:], start=True, stop=True)
 
         def count_transpose():
             if state["spare"] is not None:
                 state["since"] = state["since"] + 1
-                if state["since"] == 12:
+                if state["since"] == FILL_EVERY:
                     state["since"] = 0
                     keep_clock()
-
-        def tp_bank(name):
-            bank = 4 + state["tp"] % 4
-            state["tp"] = state["tp"] + 1
-            return psum.tile([P, 8 * P], BF16, name=name, tag="bk%d" % bank)
 
         def gram_blocks(b0, b1):
             for b in range(b0, b1):
@@ -118,76 +125,74 @@ def tile_norm_conv_kernel(tc, a, conv_kernel, out):
                     blk = a_raw[:, t, b * P : (b + 1) * P]
                     nc.tensor.matmul(out=s1p[:, b, :], lhsT=blk, rhs=ones2[:], start=(t == 0), stop=(t == PACK - 1))
 
-        def regroup_a(r0, r1):
-            nc.vector.tensor_copy(out=a_gp[:, r0:r1, 1 : W + 1, :], in_=a_rjt[:, r0:r1, :, :])
-            nc.vector.tensor_copy(out=a_gp[:, r0:r1, 0 : W + 2 : W + 1, :], in_=a_gp[:, r0:r1, 2 : W : W - 3, :])
+        def regroup_a(x):
+            if x == 0:
+                nc.vector.tensor_copy(out=a_gp[:, 1 : HALF + 2, 1 : W + 1, 0, :], in_=a_rjt[:, 0 : HALF + 1, :, :])
+                nc.vector.tensor_copy(out=a_gp[:, 0, 1 : W + 1, 0, :], in_=a_rjt[:, 1, :, :])
+            else:
+                nc.vector.tensor_copy(out=a_gp[:, 0 : HALF + 1, 1 : W + 1, 1, :], in_=a_rjt[:, HALF - 1 : H, :, :])
+                nc.vector.tensor_copy(out=a_gp[:, HALF + 1, 1 : W + 1, 1, :], in_=a_rjt[:, H - 2, :, :])
 
-        def square_sums(b0, b1):
+        def pad_columns():
+            nc.vector.tensor_copy(out=a_gp[:, :, 0 : W + 2 : W + 1, :, :], in_=a_gp[:, :, 2 : W : W - 3, :, :])
+
+        def square_sums():
             for h in range(2):
-                lo = max(b0, 4 * h)
-                hi = min(b1, 4 * h + 4)
-                if lo < hi:
-                    nc.vector.tensor_tensor(
-                        out=diag[:, lo - b0 : hi - b0, :],
-                        in0=gram[h][:, lo - 4 * h : hi - 4 * h, :],
-                        in1=ident_f[:].unsqueeze(1).to_broadcast([P, hi - lo, P]),
-                        op=ALU.mult,
-                    )
-            nc.vector.tensor_reduce(out=sums[:, b0:b1, 1], in_=diag[:, 0 : b1 - b0, :], axis=AX.X, op=ALU.add)
+                nc.vector.tensor_tensor(
+                    out=diag[:, 4 * h : 4 * h + 4, :],
+                    in0=gram[h][:],
+                    in1=ident_f[:].unsqueeze(1).to_broadcast([P, 4, P]),
+                    op=ALU.mult,
+                )
+            nc.vector.tensor_reduce(out=sums[:, :, 1], in_=diag[:], axis=AX.X, op=ALU.add)
+            nc.vector.tensor_copy(out=sums[:, :, 0], in_=s1p[:, :, 0])
 
-        def plain_sums(b0, b1):
-            nc.vector.tensor_copy(out=sums[:, b0:b1, 0], in_=s1p[:, b0:b1, 0])
-
-        def row_sums(b0, b1):
+        def row_sums():
             for q in range(4):
                 nc.tensor.matmul(
-                    out=hs[:, q, b0:b1, :].rearrange("p b s -> p (b s)"),
+                    out=hs[:, q, :, :].rearrange("p b s -> p (b s)"),
                     lhsT=spread[:, q, :, :].rearrange("p j t -> p (j t)"),
-                    rhs=sums[:, b0:b1, :].rearrange("p b s -> p (b s)"),
+                    rhs=sums[:].rearrange("p b s -> p (b s)"),
                     start=True,
                     stop=True,
                 )
 
-        def fetch_row_sums(b0, b1):
+        def variance():
             nc.vector.tensor_copy(
-                out=hpad[:, :, 1 + 4 * b0 : 1 + 4 * b1].rearrange("p s (b q) -> p s b q", q=4),
-                in_=hs[:, :, b0:b1, :].rearrange("p q b s -> p s b q"),
+                out=hpad[:, :, 1 : H + 1].rearrange("p s (b q) -> p s b q", q=4),
+                in_=hs[:].rearrange("p q b s -> p s b q"),
             )
-
-        def variance(r0, r1, pad_to, pad_from):
-            nc.vector.tensor_copy(out=hpad[:, :, pad_to : pad_to + 1], in_=hpad[:, :, pad_from : pad_from + 1])
-            nc.vector.tensor_add(out=box[:, :, r0:r1], in0=hpad[:, :, r0:r1], in1=hpad[:, :, r0 + 1 : r1 + 1])
-            nc.vector.tensor_add(out=box[:, :, r0:r1], in0=box[:, :, r0:r1], in1=hpad[:, :, r0 + 2 : r1 + 2])
+            nc.vector.tensor_copy(out=hpad[:, :, 0 : H + 2 : H + 1], in_=hpad[:, :, 2 : H : H - 3])
+            nc.vector.tensor_scalar_mul(out=hsel[:], in0=hpad[:, :, HALF : H + 2], scalar1=is_x[:, 1:2])
             nc.vector.scalar_tensor_tensor(
-                out=dev[:, r0:r1],
-                in0=box[:, 0, r0:r1],
-                scalar=1.0 / NPATCH,
-                in1=box[:, 0, r0:r1],
-                op0=ALU.mult,
-                op1=ALU.mult,
+                out=hsel[:], in0=hpad[:, :, 0 : HALF + 2], scalar=is_x[:, 0:1], in1=hsel[:], op0=ALU.mult, op1=ALU.add
             )
-            nc.vector.tensor_sub(out=dev[:, r0:r1], in0=box[:, 1, r0:r1], in1=dev[:, r0:r1])
-            nc.scalar.activation(out=std[:, r0:r1], in_=dev[:, r0:r1], func=ACT.Sqrt, scale=1.0 / (NPATCH - 1))
-            nc.vector.tensor_scalar_mul(out=mean[:, r0:r1], in0=box[:, 0, r0:r1], scalar1=1.0 / NPATCH)
+            nc.vector.tensor_add(out=box[:], in0=hsel[:, :, 0:HALF], in1=hsel[:, :, 1 : HALF + 1])
+            nc.vector.tensor_add(out=box[:], in0=box[:], in1=hsel[:, :, 2 : HALF + 2])
+            nc.vector.scalar_tensor_tensor(
+                out=dev[:], in0=box[:, 0, :], scalar=1.0 / NPATCH, in1=box[:, 0, :], op0=ALU.mult, op1=ALU.mult
+            )
+            nc.vector.tensor_sub(out=dev[:], in0=box[:, 1, :], in1=dev[:])
+            nc.scalar.activation(out=std[:], in_=dev[:], func=ACT.Sqrt, scale=1.0 / (NPATCH - 1))
+            nc.vector.tensor_scalar_mul(out=mean[:], in0=box[:, 0, :], scalar1=1.0 / NPATCH)
 
-        def inverse_std(r0, r1):
-            nc.vector.reciprocal(out=rstd[:, r0:r1], in_=std[:, r0:r1])
+        def inverse_std():
+            nc.vector.reciprocal(out=rstd[:], in_=std[:])
 
         def forward(g0, g1):
             for g in range(g0, g1):
-                first = g * 8
-                cnt = min(8, n_fwd - first)
+                first = g * 4
+                cnt = min(4, n_fwd - first)
                 pt = tp_bank("pt")
                 for u in range(cnt):
-                    prow, kw = divmod(first + u, 3)
-                    row = 1 if prow == 0 else (H - 2 if prow == H + 1 else prow - 1)
+                    srow, kw = divmod(first + u, 3)
                     nc.tensor.transpose(
                         pt[:, u * P : (u + 1) * P],
-                        a_gp[:, row, kw : kw + W, :].rearrange("p j t -> p (j t)"),
-                        ident_b[:],
+                        a_gp[:, srow, kw : kw + W, :, :].rearrange("p j x t -> p (j x t)").bitcast(F32),
+                        ident_f[:],
                     )
                     count_transpose()
-                nc.scalar.copy(out=a_t[:, first * P : (first + cnt) * P].bitcast(F32), in_=pt[:, 0 : cnt * P].bitcast(F32))
+                nc.scalar.copy(out=a_t[:, first * TILE : (first + cnt) * TILE].bitcast(F32), in_=pt[:, 0 : cnt * P])
 
         def regroup_w(eng, tap, o0, o1):
             kh, kw = divmod(tap, 3)
@@ -205,13 +210,14 @@ def tile_norm_conv_kernel(tc, a, conv_kernel, out):
 
         nrm = {}
 
-        def normalise(blk):
-            nrm[blk] = nrmp.tile([P, BLK_ROWS, TAPS * P], BF16, name="nrm")
-            for rr in range(BLK_ROWS):
-                r = blk * BLK_ROWS + rr
+        def normalise(r0, r1):
+            for r in range(r0, r1):
+                blk, rr = divmod(r, BLK_PAIRS)
+                if rr == 0:
+                    nrm[blk] = nrmp.tile([P, BLK_PAIRS, TAPS * TILE], BF16, name="nrm")
                 nc.vector.tensor_scalar(
                     out=nrm[blk][:, rr, :],
-                    in0=a_t[:, r * 3 * P : (r * 3 + TAPS) * P],
+                    in0=a_t[:, r * 3 * TILE : (r * 3 + TAPS) * TILE],
                     scalar1=mean[:, r : r + 1],
                     scalar2=rstd[:, r : r + 1],
                     op0=ALU.subtract,
@@ -222,21 +228,23 @@ def tile_norm_conv_kernel(tc, a, conv_kernel, out):
         codes = {}
         scales = {}
 
-        def backward(unit, by_rows):
+        def backward(unit, by_pairs):
             blk, kh = divmod(unit, 3)
             banks = [tp_bank("pb%d" % i) for i in range(3)]
-            order = [(rr, i) for rr in range(BLK_ROWS) for i in range(3)]
-            if not by_rows:
-                order = [(rr, i) for i in range(3) for rr in range(BLK_ROWS)]
+            order = [(rr, i) for rr in range(BLK_PAIRS) for i in range(3)]
+            if not by_pairs:
+                order = [(rr, i) for i in range(3) for rr in range(BLK_PAIRS)]
             for rr, i in order:
                 tap = kh * 3 + i
                 nc.tensor.transpose(
-                    banks[i][:, rr * P : (rr + 1) * P], nrm[blk][:, rr, tap * P : (tap + 1) * P], ident_b[:]
+                    banks[i][:, rr * P : (rr + 1) * P],
+                    nrm[blk][:, rr, tap * TILE : (tap + 1) * TILE].bitcast(F32),
+                    ident_f[:],
                 )
                 count_transpose()
             grp[unit] = grpp.tile([P, 3, BLK_PIX * PACK], BF16, name="grp", align_bytes=64)
             for i in range(3):
-                nc.scalar.copy(out=grp[unit][:, i, :].bitcast(F32), in_=banks[i][:].bitcast(F32))
+                nc.scalar.copy(out=grp[unit][:, i, :].bitcast(F32), in_=banks[i][:])
 
         def quantise(unit):
             codes[unit] = codep.tile([P, 3, BLK_PIX], U32, name="codes", align_bytes=64)
@@ -267,74 +275,75 @@ def tile_norm_conv_kernel(tc, a, conv_kernel, out):
                         stop=(tap == TAPS - 1),
                     )
                 if kh == 2:
-                    res = resp.tile([P, BLK_PIX], F32, name="res")
-                    nc.scalar.copy(out=res[:], in_=acc[ot][:])
-                    nc.sync.dma_start(out=out_v[:, ot, blk * BLK_PIX : (blk + 1) * BLK_PIX], in_=res[:])
+                    res = resp.tile([P, 2, BLK_PAIRS, W], F32, name="res")
+                    nc.scalar.copy(out=res[:], in_=acc[ot][:].rearrange("p (r j x) -> p x r j", j=W, x=2))
+                    nc.sync.dma_start(
+                        out=out_v[:, ot, :, blk * BLK_PAIRS * W : (blk + 1) * BLK_PAIRS * W],
+                        in_=res[:].rearrange("p x r j -> p x (r j)"),
+                    )
 
         state["spare"] = psum.tile([P, 512], F32, name="spare_a", tag="bk7")
         for i in range(3):
             keep_clock()
-        gram_blocks(0, 5)
-        regroup_a(0, ROWS_A)
-        regroup_a(ROWS_A, H)
-        square_sums(0, 5)
-        plain_sums(0, 5)
+        gram_blocks(0, 4)
+        gram_blocks(4, 8)
+        regroup_a(0)
+        regroup_a(1)
+        pad_columns()
+        square_sums()
         state["spare"] = psum.tile([P, 512], F32, name="spare_b", tag="bk0")
         regroup_w("s", 2, 0, O // 2)
-        forward(0, 4)
-        row_sums(0, 5)
+        forward(0, 5)
+        row_sums()
         regroup_w("v", 0, 0, O)
         regroup_w("v", 1, 0, O)
+        regroup_w("s", 2, O // 2, O)
+        variance()
         quantise_w(0)
         quantise_w(1)
-        regroup_w("s", 2, O // 2, O)
-        fetch_row_sums(0, 5)
-        variance(0, 16, 0, 2)
-        gram_blocks(5, 8)
-        square_sums(5, 8)
-        inverse_std(0, 16)
+        inverse_std()
+        forward(5, 8)
+        normalise(0, 4)
         regroup_w("s", 5, 0, O // 2)
-        forward(4, 7)
-        normalise(0)
         regroup_w("s", 5, O // 2, O)
         regroup_w("s", 7, 0, O // 2)
+        keep_clock()
+        keep_clock()
         backward(0, True)
-        plain_sums(5, 8)
         quantise_w(2)
-        normalise(1)
-        backward(1, False)
-        backward(2, False)
-        row_sums(5, 8)
-        quantise(0)
         regroup_w("v", 3, 0, O)
         regroup_w("v", 4, 0, O)
-        fetch_row_sums(5, 8)
+        normalise(4, 5)
+        backward(1, False)
+        backward(2, False)
+        quantise(0)
+        normalise(5, 8)
         quantise(1)
         quantise_w(3)
         quantise_w(4)
         quantise_w(5)
         regroup_w("v", 6, 0, O)
         quantise(2)
+        forward(8, 10)
         regroup_w("s", 7, O // 2, O)
-        forward(7, 10)
         regroup_w("s", 8, 0, O // 2)
         regroup_w("s", 8, O // 2, O)
+        forward(10, 11)
         quantise_w(6)
         quantise_w(7)
         quantise_w(8)
-
         state["spare"] = None
 
         for slot in range(LAG, N_UNITS + LAG):
             if slot == 6:
-                forward(10, 13)
-                normalise(3)
+                forward(11, 14)
             multiply(slot - LAG)
             if slot < N_UNITS:
                 backward(slot, False)
+                if slot == 3:
+                    normalise(8, 9)
                 if slot == 4:
-                    variance(16, H, H + 1, H - 1)
+                    normalise(9, 12)
+                if slot == 6:
+                    normalise(12, 16)
                 quantise(slot)
-            if slot == 4:
-                inverse_std(16, H)
-                normalise(2)

@@ -22,11 +22,19 @@ PIX = H * W
 HALF = H // 2
 BLK_PAIRS = 4
 BLK_PIX = BLK_PAIRS * 2 * W
-N_UNITS = 12
+N_BLOCKS = HALF // BLK_PAIRS
+N_UNITS = 3 * N_BLOCKS
 LAG = 3
 TILE = 2 * P
+N_FORWARD = (HALF + 2) * 3
+PER_BANK = 4
 FILL_EVERY = 8
 FLOPS = 2 * PIX * NPATCH * O
+
+
+def forward_groups(block):
+    last_pair = block * BLK_PAIRS + BLK_PAIRS - 1
+    return (3 * last_pair + TAPS - 1) // PER_BANK + 1
 
 
 def tile_norm_conv_kernel(tc, a, conv_kernel, out):
@@ -56,11 +64,11 @@ def tile_norm_conv_kernel(tc, a, conv_kernel, out):
         a_raw = keep.tile([P, PACK, PIX], BF16, name="a_raw")
         nc.sync.dma_start(out=a_raw[:, :, 0:pix_a], in_=a_v[:, :, 0:pix_a])
         nc.sync.dma_start(out=a_raw[:, :, pix_a:PIX], in_=a_v[:, :, pix_a:PIX])
-        w_raw = []
-        for kh in range(3):
-            wr = keep.tile([P, PACK, 3 * O], BF16, name="w_raw%d" % kh)
-            nc.sync.dma_start(out=wr[:], in_=w_v[:, :, kh * 3 * O : (kh + 1) * 3 * O])
-            w_raw.append(wr)
+        w_raw = [keep.tile([P, PACK, 3 * O], BF16, name="w_raw%d" % kh) for kh in range(3)]
+        for tap in (2, 0, 1):
+            nc.sync.dma_start(out=w_raw[0][:, :, tap * O : (tap + 1) * O], in_=w_v[:, :, tap * O : (tap + 1) * O])
+        for kh in (1, 2):
+            nc.sync.dma_start(out=w_raw[kh][:], in_=w_v[:, :, kh * 3 * O : (kh + 1) * 3 * O])
 
         eye3 = ident_f[:].rearrange("p (q j) -> p q j", j=W)
         band = keep.tile([P, 4, W], F32, name="band")
@@ -78,8 +86,7 @@ def tile_norm_conv_kernel(tc, a, conv_kernel, out):
 
         a_gp = keep.tile([P, HALF + 2, W + 2, 2, PACK], BF16, name="a_gp")
         a_rjt = a_raw[:].rearrange("p t (r j) -> p r j t", j=W)
-        n_fwd = (HALF + 2) * 3
-        a_t = keep.tile([P, n_fwd * TILE], BF16, name="a_t")
+        a_t = keep.tile([P, N_FORWARD * TILE], BF16, name="a_t")
         sums = keep.tile([P, 8, 2], F32, name="sums")
         diag = keep.tile([P, 8, P], F32, name="diag")
         hpad = keep.tile([P, 2, H + 2], F32, name="hpad")
@@ -98,10 +105,10 @@ def tile_norm_conv_kernel(tc, a, conv_kernel, out):
         hs = psum.tile([P, 4, 8, 2], F32, name="hs", tag="bk3")
         state = {"tp": 0, "since": 0, "spare": None}
 
-        def tp_bank(name):
+        def transpose_bank(name):
             bank = 4 + state["tp"] % 4
             state["tp"] = state["tp"] + 1
-            return psum.tile([P, 4 * P], F32, name=name, tag="bk%d" % bank)
+            return psum.tile([P, PER_BANK * P], F32, name=name, tag="bk%d" % bank)
 
         def keep_clock():
             nc.tensor.matmul(out=state["spare"][:], lhsT=ident_b[:], rhs=filler[:], start=True, stop=True)
@@ -113,17 +120,17 @@ def tile_norm_conv_kernel(tc, a, conv_kernel, out):
                     state["since"] = 0
                     keep_clock()
 
-        def gram_blocks(b0, b1):
+        def channel_sums(b0, b1):
             for b in range(b0, b1):
                 for t in range(PACK):
-                    blk = a_raw[:, t, b * P : (b + 1) * P]
+                    slab = a_raw[:, t, b * P : (b + 1) * P]
                     nc.tensor.matmul(
-                        out=gram[b // 4][:, b % 4, :], lhsT=blk, rhs=blk, start=(t == 0), stop=(t == PACK - 1)
+                        out=gram[b // 4][:, b % 4, :], lhsT=slab, rhs=slab, start=(t == 0), stop=(t == PACK - 1)
                     )
             for b in range(b0, b1):
                 for t in range(PACK):
-                    blk = a_raw[:, t, b * P : (b + 1) * P]
-                    nc.tensor.matmul(out=s1p[:, b, :], lhsT=blk, rhs=ones2[:], start=(t == 0), stop=(t == PACK - 1))
+                    slab = a_raw[:, t, b * P : (b + 1) * P]
+                    nc.tensor.matmul(out=s1p[:, b, :], lhsT=slab, rhs=ones2[:], start=(t == 0), stop=(t == PACK - 1))
 
         def regroup_a(x):
             if x == 0:
@@ -136,7 +143,7 @@ def tile_norm_conv_kernel(tc, a, conv_kernel, out):
         def pad_columns():
             nc.vector.tensor_copy(out=a_gp[:, :, 0 : W + 2 : W + 1, :, :], in_=a_gp[:, :, 2 : W : W - 3, :, :])
 
-        def square_sums():
+        def collect_sums():
             for h in range(2):
                 nc.vector.tensor_tensor(
                     out=diag[:, 4 * h : 4 * h + 4, :],
@@ -157,7 +164,7 @@ def tile_norm_conv_kernel(tc, a, conv_kernel, out):
                     stop=True,
                 )
 
-        def variance():
+        def mean_and_std():
             nc.vector.tensor_copy(
                 out=hpad[:, :, 1 : H + 1].rearrange("p s (b q) -> p s b q", q=4),
                 in_=hs[:].rearrange("p q b s -> p s b q"),
@@ -181,24 +188,24 @@ def tile_norm_conv_kernel(tc, a, conv_kernel, out):
 
         def forward(g0, g1):
             for g in range(g0, g1):
-                first = g * 4
-                cnt = min(4, n_fwd - first)
-                pt = tp_bank("pt")
-                for u in range(cnt):
-                    srow, kw = divmod(first + u, 3)
+                first = g * PER_BANK
+                cnt = min(PER_BANK, N_FORWARD - first)
+                pt = transpose_bank("pt")
+                for k in range(cnt):
+                    s, kw = divmod(first + k, 3)
                     nc.tensor.transpose(
-                        pt[:, u * P : (u + 1) * P],
-                        a_gp[:, srow, kw : kw + W, :, :].rearrange("p j x t -> p (j x t)").bitcast(F32),
+                        pt[:, k * P : (k + 1) * P],
+                        a_gp[:, s, kw : kw + W, :, :].rearrange("p j x t -> p (j x t)").bitcast(F32),
                         ident_f[:],
                     )
                     count_transpose()
                 nc.scalar.copy(out=a_t[:, first * TILE : (first + cnt) * TILE].bitcast(F32), in_=pt[:, 0 : cnt * P])
 
-        def regroup_w(eng, tap, o0, o1):
+        def regroup_w(engine, tap, o0, o1):
             kh, kw = divmod(tap, 3)
             src = w_raw[kh][:, :, kw * O + o0 : kw * O + o1].rearrange("p t (c i) -> p c t i", i=4)
             dst = wg[tap][:, o0 * PACK : o1 * PACK].rearrange("p (c i t) -> p c t i", i=4, t=PACK)
-            if eng == "v":
+            if engine == "vector":
                 nc.vector.tensor_copy(out=dst, in_=src)
             else:
                 nc.scalar.copy(out=dst, in_=src)
@@ -212,11 +219,11 @@ def tile_norm_conv_kernel(tc, a, conv_kernel, out):
 
         def normalise(r0, r1):
             for r in range(r0, r1):
-                blk, rr = divmod(r, BLK_PAIRS)
+                block, rr = divmod(r, BLK_PAIRS)
                 if rr == 0:
-                    nrm[blk] = nrmp.tile([P, BLK_PAIRS, TAPS * TILE], BF16, name="nrm")
+                    nrm[block] = nrmp.tile([P, BLK_PAIRS, TAPS * TILE], BF16, name="nrm")
                 nc.vector.tensor_scalar(
-                    out=nrm[blk][:, rr, :],
+                    out=nrm[block][:, rr, :],
                     in0=a_t[:, r * 3 * TILE : (r * 3 + TAPS) * TILE],
                     scalar1=mean[:, r : r + 1],
                     scalar2=rstd[:, r : r + 1],
@@ -229,8 +236,8 @@ def tile_norm_conv_kernel(tc, a, conv_kernel, out):
         scales = {}
 
         def backward(unit, by_pairs):
-            blk, kh = divmod(unit, 3)
-            banks = [tp_bank("pb%d" % i) for i in range(3)]
+            block, kh = divmod(unit, 3)
+            banks = [transpose_bank("pb%d" % i) for i in range(3)]
             order = [(rr, i) for rr in range(BLK_PAIRS) for i in range(3)]
             if not by_pairs:
                 order = [(rr, i) for i in range(3) for rr in range(BLK_PAIRS)]
@@ -238,7 +245,7 @@ def tile_norm_conv_kernel(tc, a, conv_kernel, out):
                 tap = kh * 3 + i
                 nc.tensor.transpose(
                     banks[i][:, rr * P : (rr + 1) * P],
-                    nrm[blk][:, rr, tap * TILE : (tap + 1) * TILE].bitcast(F32),
+                    nrm[block][:, rr, tap * TILE : (tap + 1) * TILE].bitcast(F32),
                     ident_f[:],
                 )
                 count_transpose()
@@ -259,7 +266,7 @@ def tile_norm_conv_kernel(tc, a, conv_kernel, out):
         acc = {}
 
         def multiply(unit):
-            blk, kh = divmod(unit, 3)
+            block, kh = divmod(unit, 3)
             for ot in range(4):
                 if kh == 0:
                     acc[ot] = psum.tile([P, BLK_PIX], F32, name="acc%d" % ot, tag="bk%d" % ot)
@@ -278,41 +285,42 @@ def tile_norm_conv_kernel(tc, a, conv_kernel, out):
                     res = resp.tile([P, 2, BLK_PAIRS, W], F32, name="res")
                     nc.scalar.copy(out=res[:], in_=acc[ot][:].rearrange("p (r j x) -> p x r j", j=W, x=2))
                     nc.sync.dma_start(
-                        out=out_v[:, ot, :, blk * BLK_PAIRS * W : (blk + 1) * BLK_PAIRS * W],
+                        out=out_v[:, ot, :, block * BLK_PAIRS * W : (block + 1) * BLK_PAIRS * W],
                         in_=res[:].rearrange("p x r j -> p x (r j)"),
                     )
 
+        half_o = O // 2
         state["spare"] = psum.tile([P, 512], F32, name="spare_a", tag="bk7")
         for i in range(3):
             keep_clock()
-        gram_blocks(0, 4)
-        gram_blocks(4, 8)
+        channel_sums(0, 4)
+        channel_sums(4, 8)
         regroup_a(0)
         regroup_a(1)
         pad_columns()
-        square_sums()
+        collect_sums()
         state["spare"] = psum.tile([P, 512], F32, name="spare_b", tag="bk0")
-        regroup_w("s", 2, 0, O // 2)
-        forward(0, 5)
+        regroup_w("scalar", 2, 0, half_o)
+        regroup_w("scalar", 2, half_o, O)
+        forward(0, forward_groups(0))
         row_sums()
-        regroup_w("v", 0, 0, O)
-        regroup_w("v", 1, 0, O)
-        regroup_w("s", 2, O // 2, O)
-        variance()
+        regroup_w("vector", 0, 0, O)
+        regroup_w("vector", 1, 0, O)
+        mean_and_std()
+        regroup_w("scalar", 5, 0, half_o)
         quantise_w(0)
         quantise_w(1)
         inverse_std()
-        forward(5, 8)
-        normalise(0, 4)
-        regroup_w("s", 5, 0, O // 2)
-        regroup_w("s", 5, O // 2, O)
-        regroup_w("s", 7, 0, O // 2)
+        forward(forward_groups(0), forward_groups(1))
+        normalise(0, BLK_PAIRS)
+        regroup_w("scalar", 5, half_o, O)
+        regroup_w("scalar", 7, 0, half_o)
         keep_clock()
         keep_clock()
         backward(0, True)
         quantise_w(2)
-        regroup_w("v", 3, 0, O)
-        regroup_w("v", 4, 0, O)
+        regroup_w("vector", 3, 0, O)
+        regroup_w("vector", 4, 0, O)
         normalise(4, 5)
         backward(1, False)
         backward(2, False)
@@ -322,28 +330,26 @@ def tile_norm_conv_kernel(tc, a, conv_kernel, out):
         quantise_w(3)
         quantise_w(4)
         quantise_w(5)
-        regroup_w("v", 6, 0, O)
+        regroup_w("vector", 6, 0, O)
         quantise(2)
-        forward(8, 10)
-        regroup_w("s", 7, O // 2, O)
-        regroup_w("s", 8, 0, O // 2)
-        regroup_w("s", 8, O // 2, O)
-        forward(10, 11)
+        forward(forward_groups(1), forward_groups(2) - 1)
+        regroup_w("scalar", 7, half_o, O)
+        regroup_w("scalar", 8, 0, half_o)
+        regroup_w("scalar", 8, half_o, O)
+        forward(forward_groups(2) - 1, forward_groups(2))
         quantise_w(6)
         quantise_w(7)
         quantise_w(8)
         state["spare"] = None
 
+        forward_in_slot = {4: forward_groups(2), 5: forward_groups(2) + 1, 6: forward_groups(2) + 2}
+        pairs_in_slot = {3: (8, 9), 4: (9, 12), 5: (12, 14), 6: (14, 16)}
         for slot in range(LAG, N_UNITS + LAG):
-            if slot == 6:
-                forward(11, 14)
             multiply(slot - LAG)
+            if slot in forward_in_slot:
+                forward(forward_in_slot[slot], forward_in_slot[slot] + 1)
             if slot < N_UNITS:
                 backward(slot, False)
-                if slot == 3:
-                    normalise(8, 9)
-                if slot == 4:
-                    normalise(9, 12)
-                if slot == 6:
-                    normalise(12, 16)
+                if slot in pairs_in_slot:
+                    normalise(pairs_in_slot[slot][0], pairs_in_slot[slot][1])
                 quantise(slot)

@@ -134,10 +134,12 @@ def tile_norm_conv_kernel(tc, a, conv_kernel, out):
 
         def regroup_a(x):
             if x == 0:
-                nc.vector.tensor_copy(out=a_gp[:, 1 : HALF + 2, 1 : W + 1, 0, :], in_=a_rjt[:, 0 : HALF + 1, :, :])
+                nc.vector.tensor_copy(out=a_gp[:, 1 : HALF + 1, 1 : W + 1, 0, :], in_=a_rjt[:, 0:HALF, :, :])
+                nc.vector.tensor_copy(out=a_gp[:, HALF + 1, 1 : W + 1, 0, :], in_=a_rjt[:, HALF, :, :])
                 nc.vector.tensor_copy(out=a_gp[:, 0, 1 : W + 1, 0, :], in_=a_rjt[:, 1, :, :])
             else:
-                nc.vector.tensor_copy(out=a_gp[:, 0 : HALF + 1, 1 : W + 1, 1, :], in_=a_rjt[:, HALF - 1 : H, :, :])
+                nc.vector.tensor_copy(out=a_gp[:, 1 : HALF + 1, 1 : W + 1, 1, :], in_=a_rjt[:, HALF:H, :, :])
+                nc.vector.tensor_copy(out=a_gp[:, 0, 1 : W + 1, 1, :], in_=a_rjt[:, HALF - 1, :, :])
                 nc.vector.tensor_copy(out=a_gp[:, HALF + 1, 1 : W + 1, 1, :], in_=a_rjt[:, H - 2, :, :])
 
         def pad_columns():

@@ -28,6 +28,8 @@ LAG = 3
 TILE = 2 * P
 N_FORWARD = (HALF + 2) * 3
 PER_BANK = 4
+SCALAR_ROWS = 8
+OH = O // 2
 FILL_EVERY = 8
 FLOPS = 2 * PIX * NPATCH * O
 
@@ -45,7 +47,7 @@ def tile_norm_conv_kernel(tc, a, conv_kernel, out):
 
     with tc.tile_pool(name="keep", bufs=1) as keep, tc.tile_pool(name="nrmp", bufs=2) as nrmp, tc.tile_pool(
         name="grpp", bufs=4
-    ) as grpp, tc.tile_pool(name="codep", bufs=5) as codep, tc.tile_pool(name="resp", bufs=4) as resp, tc.psum_pool(
+    ) as grpp, tc.tile_pool(name="codep", bufs=8) as codep, tc.tile_pool(name="wgp", bufs=8) as wgp, tc.tile_pool(name="resp", bufs=4) as resp, tc.psum_pool(
         name="psum", bufs=1
     ) as psum, tc.manual_schedule():
         filler = keep.tile([P, 512], BF16, name="filler")
@@ -89,7 +91,6 @@ def tile_norm_conv_kernel(tc, a, conv_kernel, out):
         a_t = keep.tile([P, N_FORWARD * TILE], BF16, name="a_t")
         sums = keep.tile([P, 8, 2], F32, name="sums")
         diag = keep.tile([P, 8, P], F32, name="diag")
-        hpad = keep.tile([P, 2, H + 2], F32, name="hpad")
         hsel = keep.tile([P, 2, HALF + 2], F32, name="hsel")
         box = keep.tile([P, 2, HALF], F32, name="box")
         mean = keep.tile([P, HALF], F32, name="mean")
@@ -98,11 +99,10 @@ def tile_norm_conv_kernel(tc, a, conv_kernel, out):
         rstd = keep.tile([P, HALF], F32, name="rstd")
         w_codes = keep.tile([P, TAPS, O], U32, name="w_codes", align_bytes=64)
         w_scales = keep.tile([P, TAPS, O], U8, name="w_scales", align_bytes=64)
-        wg = [keep.tile([P, O * PACK], BF16, name="wg%d" % tap, align_bytes=64) for tap in range(TAPS)]
 
         gram = [psum.tile([P, 4, P], F32, name="gram%d" % h, tag="bk%d" % h) for h in range(2)]
         s1p = psum.tile([P, 8, 2], F32, name="s1p", tag="bk2")
-        hs = psum.tile([P, 4, 8, 2], F32, name="hs", tag="bk3")
+        hs = psum.tile([P, 8, 4, 2], F32, name="hs", tag="bk3")
         state = {"tp": 0, "since": 0, "spare": None}
 
         def transpose_bank(name):
@@ -138,44 +138,46 @@ def tile_norm_conv_kernel(tc, a, conv_kernel, out):
                 nc.vector.tensor_copy(out=a_gp[:, HALF + 1, 1 : W + 1, 0, :], in_=a_rjt[:, HALF, :, :])
                 nc.vector.tensor_copy(out=a_gp[:, 0, 1 : W + 1, 0, :], in_=a_rjt[:, 1, :, :])
             else:
-                nc.vector.tensor_copy(out=a_gp[:, 1 : HALF + 1, 1 : W + 1, 1, :], in_=a_rjt[:, HALF:H, :, :])
+                mid = HALF - SCALAR_ROWS
+                nc.vector.tensor_copy(out=a_gp[:, 1 : mid + 1, 1 : W + 1, 1, :], in_=a_rjt[:, HALF : HALF + mid, :, :])
+                nc.scalar.copy(out=a_gp[:, mid + 1 : HALF + 1, 1 : W + 1, 1, :], in_=a_rjt[:, HALF + mid : H, :, :])
                 nc.vector.tensor_copy(out=a_gp[:, 0, 1 : W + 1, 1, :], in_=a_rjt[:, HALF - 1, :, :])
                 nc.vector.tensor_copy(out=a_gp[:, HALF + 1, 1 : W + 1, 1, :], in_=a_rjt[:, H - 2, :, :])
 
         def pad_columns():
             nc.vector.tensor_copy(out=a_gp[:, :, 0 : W + 2 : W + 1, :, :], in_=a_gp[:, :, 2 : W : W - 3, :, :])
 
-        def collect_sums():
-            for h in range(2):
-                nc.vector.tensor_tensor(
-                    out=diag[:, 4 * h : 4 * h + 4, :],
-                    in0=gram[h][:],
-                    in1=ident_f[:].unsqueeze(1).to_broadcast([P, 4, P]),
-                    op=ALU.mult,
-                )
-            nc.vector.tensor_reduce(out=sums[:, :, 1], in_=diag[:], axis=AX.X, op=ALU.add)
-            nc.vector.tensor_copy(out=sums[:, :, 0], in_=s1p[:, :, 0])
+        def squares(h):
+            half = slice(4 * h, 4 * h + 4)
+            nc.vector.tensor_tensor(
+                out=diag[:, half, :], in0=gram[h][:], in1=ident_f[:].unsqueeze(1).to_broadcast([P, 4, P]), op=ALU.mult
+            )
+            nc.vector.tensor_reduce(out=sums[:, half, 1], in_=diag[:, half, :], axis=AX.X, op=ALU.add)
 
         def row_sums():
             for q in range(4):
                 nc.tensor.matmul(
-                    out=hs[:, q, :, :].rearrange("p b s -> p (b s)"),
+                    out=hs[:, :, q, :],
                     lhsT=spread[:, q, :, :].rearrange("p j t -> p (j t)"),
-                    rhs=sums[:].rearrange("p b s -> p (b s)"),
+                    rhs=sums[:],
                     start=True,
                     stop=True,
                 )
 
         def mean_and_std():
-            nc.vector.tensor_copy(
-                out=hpad[:, :, 1 : H + 1].rearrange("p s (b q) -> p s b q", q=4),
-                in_=hs[:].rearrange("p q b s -> p s b q"),
-            )
-            nc.vector.tensor_copy(out=hpad[:, :, 0 : H + 2 : H + 1], in_=hpad[:, :, 2 : H : H - 3])
-            nc.vector.tensor_scalar_mul(out=hsel[:], in0=hpad[:, :, HALF : H + 2], scalar1=is_x[:, 1:2])
-            nc.vector.scalar_tensor_tensor(
-                out=hsel[:], in0=hpad[:, :, 0 : HALF + 2], scalar=is_x[:, 0:1], in1=hsel[:], op0=ALU.mult, op1=ALU.add
-            )
+            rows = hs[:].rearrange("p b q s -> p s (b q)")
+            last = HALF + 1
+            nc.vector.tensor_scalar_mul(out=hsel[:, :, 0:last], in0=rows[:, :, HALF - 1 : H], scalar1=is_x[:, 1:2])
+            nc.vector.tensor_scalar_mul(out=hsel[:, :, last:], in0=rows[:, :, H - 2 : H - 1], scalar1=is_x[:, 1:2])
+            for e0, e1, row in ((1, HALF + 2, 0), (0, 1, 1)):
+                nc.vector.scalar_tensor_tensor(
+                    out=hsel[:, :, e0:e1],
+                    in0=rows[:, :, row : row + e1 - e0],
+                    scalar=is_x[:, 0:1],
+                    in1=hsel[:, :, e0:e1],
+                    op0=ALU.mult,
+                    op1=ALU.add,
+                )
             nc.vector.tensor_add(out=box[:], in0=hsel[:, :, 0:HALF], in1=hsel[:, :, 1 : HALF + 1])
             nc.vector.tensor_add(out=box[:], in0=box[:], in1=hsel[:, :, 2 : HALF + 2])
             nc.vector.scalar_tensor_tensor(
@@ -188,72 +190,82 @@ def tile_norm_conv_kernel(tc, a, conv_kernel, out):
         def inverse_std():
             nc.vector.reciprocal(out=rstd[:], in_=std[:])
 
-        def forward(g0, g1):
-            for g in range(g0, g1):
-                first = g * PER_BANK
-                cnt = min(PER_BANK, N_FORWARD - first)
-                pt = transpose_bank("pt")
-                for k in range(cnt):
-                    s, kw = divmod(first + k, 3)
-                    nc.tensor.transpose(
-                        pt[:, k * P : (k + 1) * P],
-                        a_gp[:, s, kw : kw + W, :, :].rearrange("p j x t -> p (j x t)").bitcast(F32),
-                        ident_f[:],
-                    )
-                    count_transpose()
-                nc.scalar.copy(out=a_t[:, first * TILE : (first + cnt) * TILE].bitcast(F32), in_=pt[:, 0 : cnt * P])
+        ahead = {}
 
-        def regroup_w(engine, tap, o0, o1):
+        def forward(g):
+            first = g * PER_BANK
+            ahead[g] = transpose_bank("pt")
+            for k in range(min(PER_BANK, N_FORWARD - first)):
+                s, kw = divmod(first + k, 3)
+                nc.tensor.transpose(
+                    ahead[g][:, k * P : (k + 1) * P],
+                    a_gp[:, s, kw : kw + W, :, :].rearrange("p j x t -> p (j x t)").bitcast(F32),
+                    ident_f[:],
+                )
+                count_transpose()
+
+        def take_forward(g):
+            first = g * PER_BANK
+            cnt = min(PER_BANK, N_FORWARD - first)
+            nc.scalar.copy(out=a_t[:, first * TILE : (first + cnt) * TILE].bitcast(F32), in_=ahead[g][:, 0 : cnt * P])
+
+        wg = {}
+
+        def regroup_w(engine, tap, oh):
+            wg[tap, oh] = wgp.tile([P, OH * PACK], BF16, name="wg", align_bytes=64)
             kh, kw = divmod(tap, 3)
-            src = w_raw[kh][:, :, kw * O + o0 : kw * O + o1].rearrange("p t (c i) -> p c t i", i=4)
-            dst = wg[tap][:, o0 * PACK : o1 * PACK].rearrange("p (c i t) -> p c t i", i=4, t=PACK)
+            first = kw * O + oh * OH
+            src = w_raw[kh][:, :, first : first + OH].rearrange("p t (c i) -> p c t i", i=4)
+            dst = wg[tap, oh][:].rearrange("p (c i t) -> p c t i", i=4, t=PACK)
             if engine == "vector":
                 nc.vector.tensor_copy(out=dst, in_=src)
             else:
                 nc.scalar.copy(out=dst, in_=src)
 
-        def quantise_w(tap):
+        def quantise_w(tap, oh):
+            half = slice(oh * OH, (oh + 1) * OH)
             nc.vector.quantize_mx(
-                out=w_codes[:, tap, :].bitcast(FP8X4), scales=w_scales[:, tap, :], in_=wg[tap][:]
+                out=w_codes[:, tap, half].bitcast(FP8X4), scales=w_scales[:, tap, half], in_=wg[tap, oh][:]
             )
 
         nrm = {}
 
-        def normalise(r0, r1):
+        def normalise(r0, r1, kh0, kh1):
             for r in range(r0, r1):
                 block, rr = divmod(r, BLK_PAIRS)
-                if rr == 0:
+                if block not in nrm:
                     nrm[block] = nrmp.tile([P, BLK_PAIRS, TAPS * TILE], BF16, name="nrm")
                 nc.vector.tensor_scalar(
-                    out=nrm[block][:, rr, :],
-                    in0=a_t[:, r * 3 * TILE : (r * 3 + TAPS) * TILE],
+                    out=nrm[block][:, rr, kh0 * 3 * TILE : kh1 * 3 * TILE],
+                    in0=a_t[:, (r + kh0) * 3 * TILE : (r + kh1) * 3 * TILE],
                     scalar1=mean[:, r : r + 1],
                     scalar2=rstd[:, r : r + 1],
                     op0=ALU.subtract,
                     op1=ALU.mult,
                 )
 
+        back = {}
         grp = {}
         codes = {}
         scales = {}
 
-        def backward(unit, by_pairs):
+        def backward(unit):
             block, kh = divmod(unit, 3)
-            banks = [transpose_bank("pb%d" % i) for i in range(3)]
-            order = [(rr, i) for rr in range(BLK_PAIRS) for i in range(3)]
-            if not by_pairs:
-                order = [(rr, i) for i in range(3) for rr in range(BLK_PAIRS)]
-            for rr, i in order:
+            for i in range(3):
                 tap = kh * 3 + i
-                nc.tensor.transpose(
-                    banks[i][:, rr * P : (rr + 1) * P],
-                    nrm[block][:, rr, tap * TILE : (tap + 1) * TILE].bitcast(F32),
-                    ident_f[:],
-                )
-                count_transpose()
+                back[unit, i] = transpose_bank("pb")
+                for rr in range(BLK_PAIRS):
+                    nc.tensor.transpose(
+                        back[unit, i][:, rr * P : (rr + 1) * P],
+                        nrm[block][:, rr, tap * TILE : (tap + 1) * TILE].bitcast(F32),
+                        ident_f[:],
+                    )
+                    count_transpose()
+
+        def take(unit):
             grp[unit] = grpp.tile([P, 3, BLK_PIX * PACK], BF16, name="grp", align_bytes=64)
             for i in range(3):
-                nc.scalar.copy(out=grp[unit][:, i, :].bitcast(F32), in_=banks[i][:])
+                nc.scalar.copy(out=grp[unit][:, i, :].bitcast(F32), in_=back[unit, i][:])
 
         def quantise(unit):
             codes[unit] = codep.tile([P, 3, BLK_PIX], U32, name="codes", align_bytes=64)
@@ -267,15 +279,16 @@ def tile_norm_conv_kernel(tc, a, conv_kernel, out):
 
         acc = {}
 
-        def multiply(unit):
+        def multiply(unit, oh):
             block, kh = divmod(unit, 3)
-            for ot in range(4):
+            for ot in (2 * oh, 2 * oh + 1):
                 if kh == 0:
-                    acc[ot] = psum.tile([P, BLK_PIX], F32, name="acc%d" % ot, tag="bk%d" % ot)
+                    bank = ot % 2 + 2 * (block if block < 2 else oh)
+                    acc[block, ot] = psum.tile([P, BLK_PIX], F32, name="acc", tag="bk%d" % bank)
                 for i in range(3):
                     tap = kh * 3 + i
                     nc.tensor.matmul_mx(
-                        out=acc[ot][:],
+                        out=acc[block, ot][:],
                         lhsT=w_codes[:, tap, ot * P : (ot + 1) * P].bitcast(FP8X4),
                         lhsT_scale=w_scales[:, tap, ot * P : (ot + 1) * P],
                         rhs=codes[unit][:, i, :].bitcast(FP8X4),
@@ -283,75 +296,166 @@ def tile_norm_conv_kernel(tc, a, conv_kernel, out):
                         start=(tap == 0),
                         stop=(tap == TAPS - 1),
                     )
-                if kh == 2:
-                    res = resp.tile([P, 2, BLK_PAIRS, W], F32, name="res")
-                    nc.scalar.copy(out=res[:], in_=acc[ot][:].rearrange("p (r j x) -> p x r j", j=W, x=2))
-                    nc.sync.dma_start(
-                        out=out_v[:, ot, :, block * BLK_PAIRS * W : (block + 1) * BLK_PAIRS * W],
-                        in_=res[:].rearrange("p x r j -> p x (r j)"),
-                    )
 
-        half_o = O // 2
+        def store(block, oh):
+            for ot in (2 * oh, 2 * oh + 1):
+                res = resp.tile([P, 2, BLK_PAIRS, W], F32, name="res")
+                nc.scalar.copy(out=res[:], in_=acc[block, ot][:].rearrange("p (r j x) -> p x r j", j=W, x=2))
+                nc.sync.dma_start(
+                    out=out_v[:, ot, :, block * BLK_PAIRS * W : (block + 1) * BLK_PAIRS * W],
+                    in_=res[:].rearrange("p x r j -> p x (r j)"),
+                )
+
         state["spare"] = psum.tile([P, 512], F32, name="spare_a", tag="bk7")
         for i in range(3):
             keep_clock()
         channel_sums(0, 4)
         channel_sums(4, 8)
         regroup_a(0)
+        squares(0)
         regroup_a(1)
         pad_columns()
-        collect_sums()
+        squares(1)
+        nc.vector.tensor_copy(out=sums[:, :, 0], in_=s1p[:, :, 0])
         state["spare"] = psum.tile([P, 512], F32, name="spare_b", tag="bk0")
-        regroup_w("scalar", 2, 0, half_o)
-        regroup_w("scalar", 2, half_o, O)
-        forward(0, forward_groups(0))
+        regroup_w("scalar", 2, 0)
+        regroup_w("scalar", 2, 1)
+        forward(0)
+        forward(1)
         row_sums()
-        regroup_w("vector", 0, 0, O)
-        regroup_w("vector", 1, 0, O)
+        take_forward(0)
+        take_forward(1)
+        for g in (2, 3):
+            forward(g)
+            take_forward(g)
         mean_and_std()
-        regroup_w("scalar", 5, 0, half_o)
-        quantise_w(0)
-        quantise_w(1)
         inverse_std()
-        forward(forward_groups(0), forward_groups(1))
-        normalise(0, BLK_PAIRS)
-        regroup_w("scalar", 5, half_o, O)
-        regroup_w("scalar", 7, 0, half_o)
-        keep_clock()
-        keep_clock()
-        backward(0, True)
-        quantise_w(2)
-        regroup_w("vector", 3, 0, O)
-        regroup_w("vector", 4, 0, O)
-        normalise(4, 5)
-        backward(1, False)
-        backward(2, False)
+        for g in (4, 5):
+            forward(g)
+            take_forward(g)
+        forward(6)
+        forward(7)
+        take_forward(6)
+        take_forward(7)
+        normalise(0, 4, 0, 1)
+        backward(0)
+        take(0)
+        regroup_w("scalar", 5, 0)
+        normalise(0, 4, 1, 3)
+        backward(1)
+        take(1)
+        regroup_w("vector", 0, 0)
+        backward(2)
+        forward(8)
+        take(2)
+        take_forward(8)
+        regroup_w("vector", 1, 0)
+        normalise(4, 8, 0, 1)
+        backward(3)
+        take(3)
+        quantise_w(0, 0)
+        quantise_w(1, 0)
+        quantise_w(2, 0)
         quantise(0)
-        normalise(5, 8)
-        quantise(1)
-        quantise_w(3)
-        quantise_w(4)
-        quantise_w(5)
-        regroup_w("vector", 6, 0, O)
-        quantise(2)
-        forward(forward_groups(1), forward_groups(2) - 1)
-        regroup_w("scalar", 7, half_o, O)
-        regroup_w("scalar", 8, 0, half_o)
-        regroup_w("scalar", 8, half_o, O)
-        forward(forward_groups(2) - 1, forward_groups(2))
-        quantise_w(6)
-        quantise_w(7)
-        quantise_w(8)
+        normalise(4, 8, 1, 3)
+        backward(4)
         state["spare"] = None
-
-        forward_in_slot = {4: forward_groups(2), 5: forward_groups(2) + 1, 6: forward_groups(2) + 2}
-        pairs_in_slot = {3: (8, 9), 4: (9, 12), 5: (12, 14), 6: (14, 16)}
-        for slot in range(LAG, N_UNITS + LAG):
-            multiply(slot - LAG)
-            if slot in forward_in_slot:
-                forward(forward_in_slot[slot], forward_in_slot[slot] + 1)
-            if slot < N_UNITS:
-                backward(slot, False)
-                if slot in pairs_in_slot:
-                    normalise(pairs_in_slot[slot][0], pairs_in_slot[slot][1])
-                quantise(slot)
+        multiply(0, 0)
+        take(4)
+        regroup_w("scalar", 7, 0)
+        regroup_w("vector", 3, 0)
+        backward(5)
+        regroup_w("vector", 4, 0)
+        quantise(1)
+        take(5)
+        regroup_w("scalar", 8, 0)
+        quantise_w(3, 0)
+        quantise_w(4, 0)
+        quantise_w(5, 0)
+        quantise(3)
+        multiply(3, 0)
+        forward(9)
+        forward(10)
+        forward(11)
+        multiply(1, 0)
+        take_forward(9)
+        take_forward(10)
+        take_forward(11)
+        regroup_w("vector", 6, 0)
+        quantise(2)
+        quantise(4)
+        multiply(4, 0)
+        forward(12)
+        forward(13)
+        take_forward(12)
+        take_forward(13)
+        quantise_w(6, 0)
+        quantise_w(7, 0)
+        quantise(5)
+        normalise(8, 12, 0, 3)
+        backward(6)
+        take(6)
+        quantise_w(8, 0)
+        multiply(2, 0)
+        multiply(5, 0)
+        backward(7)
+        store(0, 0)
+        regroup_w("scalar", 5, 1)
+        store(1, 0)
+        take(7)
+        regroup_w("scalar", 8, 1)
+        regroup_w("vector", 0, 1)
+        regroup_w("vector", 1, 1)
+        quantise_w(0, 1)
+        quantise_w(1, 1)
+        quantise_w(2, 1)
+        multiply(0, 1)
+        multiply(3, 1)
+        regroup_w("vector", 3, 1)
+        regroup_w("vector", 4, 1)
+        quantise_w(3, 1)
+        quantise_w(4, 1)
+        regroup_w("vector", 6, 1)
+        regroup_w("vector", 7, 1)
+        quantise_w(5, 1)
+        multiply(1, 1)
+        multiply(4, 1)
+        quantise_w(6, 1)
+        quantise_w(7, 1)
+        quantise(6)
+        quantise_w(8, 1)
+        multiply(2, 1)
+        multiply(5, 1)
+        backward(8)
+        store(0, 1)
+        store(1, 1)
+        take(8)
+        normalise(12, 13, 0, 3)
+        multiply(6, 0)
+        normalise(13, 16, 0, 3)
+        backward(9)
+        multiply(6, 1)
+        take(9)
+        quantise(7)
+        multiply(7, 0)
+        backward(10)
+        multiply(7, 1)
+        take(10)
+        quantise(8)
+        multiply(8, 0)
+        multiply(8, 1)
+        backward(11)
+        store(2, 0)
+        store(2, 1)
+        take(11)
+        quantise(9)
+        multiply(9, 0)
+        multiply(9, 1)
+        quantise(10)
+        multiply(10, 0)
+        multiply(10, 1)
+        quantise(11)
+        multiply(11, 0)
+        multiply(11, 1)
+        store(3, 0)
+        store(3, 1)

@@ -30,7 +30,6 @@ N_FORWARD = (HALF + 2) * 3
 PER_BANK = 4
 SCALAR_ROWS = 8
 OH = O // 2
-FILL_EVERY = 8
 FLOPS = 2 * PIX * NPATCH * O
 
 
@@ -50,10 +49,6 @@ def tile_norm_conv_kernel(tc, a, conv_kernel, out):
     ) as grpp, tc.tile_pool(name="codep", bufs=8) as codep, tc.tile_pool(name="wgp", bufs=8) as wgp, tc.tile_pool(name="resp", bufs=4) as resp, tc.psum_pool(
         name="psum", bufs=1
     ) as psum, tc.manual_schedule():
-        filler = keep.tile([P, 512], BF16, name="filler")
-        nc.vector.memset(filler[:], 0.0)
-        ident_b = keep.tile([P, P], BF16, name="ident_b")
-        make_identity(nc, ident_b[:])
         ident_f = keep.tile([P, P], F32, name="ident_f")
         make_identity(nc, ident_f[:])
         ones2 = keep.tile([P, 2], BF16, name="ones2")
@@ -103,22 +98,12 @@ def tile_norm_conv_kernel(tc, a, conv_kernel, out):
         gram = [psum.tile([P, 4, P], F32, name="gram%d" % h, tag="bk%d" % h) for h in range(2)]
         s1p = psum.tile([P, 8, 2], F32, name="s1p", tag="bk2")
         hs = psum.tile([P, 8, 4, 2], F32, name="hs", tag="bk3")
-        state = {"tp": 0, "since": 0, "spare": None}
+        state = {"tp": 0}
 
         def transpose_bank(name):
             bank = 4 + state["tp"] % 4
             state["tp"] = state["tp"] + 1
             return psum.tile([P, PER_BANK * P], F32, name=name, tag="bk%d" % bank)
-
-        def keep_clock():
-            nc.tensor.matmul(out=state["spare"][:], lhsT=ident_b[:], rhs=filler[:], start=True, stop=True)
-
-        def count_transpose():
-            if state["spare"] is not None:
-                state["since"] = state["since"] + 1
-                if state["since"] == FILL_EVERY:
-                    state["since"] = 0
-                    keep_clock()
 
         def channel_sums(b0, b1):
             for b in range(b0, b1):
@@ -202,7 +187,6 @@ def tile_norm_conv_kernel(tc, a, conv_kernel, out):
                     a_gp[:, s, kw : kw + W, :, :].rearrange("p j x t -> p (j x t)").bitcast(F32),
                     ident_f[:],
                 )
-                count_transpose()
 
         def take_forward(g):
             first = g * PER_BANK
@@ -260,7 +244,6 @@ def tile_norm_conv_kernel(tc, a, conv_kernel, out):
                         nrm[block][:, rr, tap * TILE : (tap + 1) * TILE].bitcast(F32),
                         ident_f[:],
                     )
-                    count_transpose()
 
         def take(unit):
             grp[unit] = grpp.tile([P, 3, BLK_PIX * PACK], BF16, name="grp", align_bytes=64)
@@ -306,9 +289,6 @@ def tile_norm_conv_kernel(tc, a, conv_kernel, out):
                     in_=res[:].rearrange("p x r j -> p x (r j)"),
                 )
 
-        state["spare"] = psum.tile([P, 512], F32, name="spare_a", tag="bk7")
-        for i in range(3):
-            keep_clock()
         channel_sums(0, 4)
         channel_sums(4, 8)
         regroup_a(0)
@@ -317,7 +297,6 @@ def tile_norm_conv_kernel(tc, a, conv_kernel, out):
         pad_columns()
         squares(1)
         nc.vector.tensor_copy(out=sums[:, :, 0], in_=s1p[:, :, 0])
-        state["spare"] = psum.tile([P, 512], F32, name="spare_b", tag="bk0")
         regroup_w("scalar", 2, 0)
         regroup_w("scalar", 2, 1)
         forward(0)
@@ -359,7 +338,6 @@ def tile_norm_conv_kernel(tc, a, conv_kernel, out):
         quantise(0)
         normalise(4, 8, 1, 3)
         backward(4)
-        state["spare"] = None
         multiply(0, 0)
         take(4)
         regroup_w("scalar", 7, 0)

@@ -28,7 +28,7 @@ LAG = 3
 TILE = 2 * P
 N_FORWARD = (HALF + 2) * 3
 PER_BANK = 4
-SCALAR_ROWS = 8
+SCALAR_ROWS = 12
 OH = O // 2
 FLOPS = 2 * PIX * NPATCH * O
 
@@ -67,27 +67,30 @@ def tile_norm_conv_kernel(tc, a, conv_kernel, out):
         for kh in (1, 2):
             nc.sync.dma_start(out=w_raw[kh][:], in_=w_v[:, :, kh * 3 * O : (kh + 1) * 3 * O])
 
-        eye3 = ident_f[:].rearrange("p (q j) -> p q j", j=W)
-        band = keep.tile([P, 4, W], F32, name="band")
-        nc.vector.tensor_copy(out=band[:], in_=eye3)
-        nc.vector.tensor_add(out=band[:, :, 1:W], in0=band[:, :, 1:W], in1=eye3[:, :, 0 : W - 1])
-        nc.vector.tensor_add(out=band[:, :, 0 : W - 1], in0=band[:, :, 0 : W - 1], in1=eye3[:, :, 1:W])
-        nc.vector.tensor_add(out=band[:, :, 0:1], in0=band[:, :, 0:1], in1=eye3[:, :, 1:2])
-        nc.vector.tensor_add(out=band[:, :, W - 1 : W], in0=band[:, :, W - 1 : W], in1=eye3[:, :, W - 2 : W - 1])
-        spread = keep.tile([P, 4, W, PACK], F32, name="spread")
-        nc.vector.tensor_copy(out=spread[:], in_=band[:].unsqueeze(3).to_broadcast([P, 4, W, PACK]))
-        is_x = keep.tile([P, 2], F32, name="is_x")
-        eye_jxu = ident_f[:].rearrange("p (j x u) -> p j x u", x=2, u=2)
+        is_q = keep.tile([P, 4], F32, name="is_q")
+        nc.vector.tensor_reduce(
+            out=is_q[:], in_=ident_f[:].rearrange("p (q j) -> p q j", j=W), axis=AX.X, op=ALU.add
+        )
+        eye = keep.tile([P, W], F32, name="eye")
+        nc.vector.tensor_reduce(out=eye[:], in_=ident_f[:].rearrange("p (q j) -> p j q", j=W), axis=AX.X, op=ALU.add)
+        band = keep.tile([P, W], F32, name="band")
+        nc.vector.tensor_copy(out=band[:], in_=eye[:])
+        nc.vector.tensor_add(out=band[:, 1:W], in0=band[:, 1:W], in1=eye[:, 0 : W - 1])
+        nc.vector.tensor_add(out=band[:, 0 : W - 1], in0=band[:, 0 : W - 1], in1=eye[:, 1:W])
+        nc.vector.tensor_add(out=band[:, 0:1], in0=band[:, 0:1], in1=eye[:, 1:2])
+        nc.vector.tensor_add(out=band[:, W - 1 : W], in0=band[:, W - 1 : W], in1=eye[:, W - 2 : W - 1])
+        spread = keep.tile([P, 2, W, 2, 2], F32, name="spread")
+        nc.vector.memset(spread[:].rearrange("p s j x u -> p (s j x u)"), 0.0)
         for x in range(2):
-            nc.vector.tensor_reduce(out=is_x[:, x : x + 1], in_=eye_jxu[:, :, x, :], axis=AX.XY, op=ALU.add)
+            nc.vector.tensor_copy(out=spread[:, x, :, x, :], in_=band[:].unsqueeze(2).to_broadcast([P, W, 2]))
 
         a_gp = keep.tile([P, HALF + 2, W + 2, 2, PACK], BF16, name="a_gp")
         a_rjt = a_raw[:].rearrange("p t (r j) -> p r j t", j=W)
         a_t = keep.tile([P, N_FORWARD * TILE], BF16, name="a_t")
         sums = keep.tile([P, 8, 2], F32, name="sums")
-        diag = keep.tile([P, 8, P], F32, name="diag")
-        hsel = keep.tile([P, 2, HALF + 2], F32, name="hsel")
-        box = keep.tile([P, 2, HALF], F32, name="box")
+        diag = keep.tile([P, 2, P], F32, name="diag")
+        own = keep.tile([P, H + 2, 2], F32, name="own")
+        three = keep.tile([P, H, 2], F32, name="three")
         mean = keep.tile([P, HALF], F32, name="mean")
         dev = keep.tile([P, HALF], F32, name="dev")
         std = keep.tile([P, HALF], F32, name="std")
@@ -97,7 +100,7 @@ def tile_norm_conv_kernel(tc, a, conv_kernel, out):
 
         gram = [psum.tile([P, 4, P], F32, name="gram%d" % h, tag="bk%d" % h) for h in range(2)]
         s1p = psum.tile([P, 8, 2], F32, name="s1p", tag="bk2")
-        hs = psum.tile([P, 8, 4, 2], F32, name="hs", tag="bk3")
+        box = psum.tile([P, 2 * HALF], F32, name="box", tag="bk3")
         state = {"tp": 0}
 
         def transpose_bank(name):
@@ -105,14 +108,16 @@ def tile_norm_conv_kernel(tc, a, conv_kernel, out):
             state["tp"] = state["tp"] + 1
             return psum.tile([P, PER_BANK * P], F32, name=name, tag="bk%d" % bank)
 
-        def channel_sums(b0, b1):
-            for b in range(b0, b1):
+        def gram_matrices(h):
+            for b in range(4 * h, 4 * h + 4):
                 for t in range(PACK):
                     slab = a_raw[:, t, b * P : (b + 1) * P]
                     nc.tensor.matmul(
-                        out=gram[b // 4][:, b % 4, :], lhsT=slab, rhs=slab, start=(t == 0), stop=(t == PACK - 1)
+                        out=gram[h][:, b % 4, :], lhsT=slab, rhs=slab, start=(t == 0), stop=(t == PACK - 1)
                     )
-            for b in range(b0, b1):
+
+        def channel_sums():
+            for b in range(8):
                 for t in range(PACK):
                     slab = a_raw[:, t, b * P : (b + 1) * P]
                     nc.tensor.matmul(out=s1p[:, b, :], lhsT=slab, rhs=ones2[:], start=(t == 0), stop=(t == PACK - 1))
@@ -133,44 +138,43 @@ def tile_norm_conv_kernel(tc, a, conv_kernel, out):
             nc.vector.tensor_copy(out=a_gp[:, :, 0 : W + 2 : W + 1, :, :], in_=a_gp[:, :, 2 : W : W - 3, :, :])
 
         def squares(h):
-            half = slice(4 * h, 4 * h + 4)
-            nc.vector.tensor_tensor(
-                out=diag[:, half, :], in0=gram[h][:], in1=ident_f[:].unsqueeze(1).to_broadcast([P, 4, P]), op=ALU.mult
-            )
-            nc.vector.tensor_reduce(out=sums[:, half, 1], in_=diag[:, half, :], axis=AX.X, op=ALU.add)
+            for b in range(4 * h, 4 * h + 4):
+                nc.vector.scalar_tensor_tensor(
+                    out=diag[:, b % 2, :],
+                    in0=gram[h][:, b % 4, :],
+                    scalar=1.0,
+                    in1=ident_f[:],
+                    op0=ALU.mult,
+                    op1=ALU.mult,
+                    accum_out=sums[:, b, 1:2],
+                )
 
-        def row_sums():
-            for q in range(4):
+        def box_sums():
+            nc.vector.tensor_tensor(
+                out=own[:, 1 : H + 1, :].rearrange("p (b q) s -> p b q s", q=4),
+                in0=sums[:].unsqueeze(2).to_broadcast([P, 8, 4, 2]),
+                in1=is_q[:].unsqueeze(1).unsqueeze(3).to_broadcast([P, 8, 4, 2]),
+                op=ALU.mult,
+            )
+            nc.vector.tensor_scalar_mul(out=own[:, 0, :], in0=sums[:, 0, :], scalar1=is_q[:, 1:2])
+            nc.vector.tensor_scalar_mul(out=own[:, H + 1, :], in0=sums[:, 7, :], scalar1=is_q[:, 2:3])
+            nc.vector.tensor_add(out=three[:], in0=own[:, 0:H, :], in1=own[:, 1 : H + 1, :])
+            nc.vector.tensor_add(out=three[:], in0=three[:], in1=own[:, 2 : H + 2, :])
+            for x in range(2):
                 nc.tensor.matmul(
-                    out=hs[:, :, q, :],
-                    lhsT=spread[:, q, :, :].rearrange("p j t -> p (j t)"),
-                    rhs=sums[:],
-                    start=True,
-                    stop=True,
+                    out=box[:],
+                    lhsT=spread[:, x, :, :, :].rearrange("p j x u -> p (j x u)"),
+                    rhs=three[:, x * HALF : (x + 1) * HALF, :].rearrange("p r s -> p (r s)"),
+                    start=(x == 0),
+                    stop=(x == 1),
                 )
 
         def mean_and_std():
-            rows = hs[:].rearrange("p b q s -> p s (b q)")
-            last = HALF + 1
-            nc.vector.tensor_scalar_mul(out=hsel[:, :, 0:last], in0=rows[:, :, HALF - 1 : H], scalar1=is_x[:, 1:2])
-            nc.vector.tensor_scalar_mul(out=hsel[:, :, last:], in0=rows[:, :, H - 2 : H - 1], scalar1=is_x[:, 1:2])
-            for e0, e1, row in ((1, HALF + 2, 0), (0, 1, 1)):
-                nc.vector.scalar_tensor_tensor(
-                    out=hsel[:, :, e0:e1],
-                    in0=rows[:, :, row : row + e1 - e0],
-                    scalar=is_x[:, 0:1],
-                    in1=hsel[:, :, e0:e1],
-                    op0=ALU.mult,
-                    op1=ALU.add,
-                )
-            nc.vector.tensor_add(out=box[:], in0=hsel[:, :, 0:HALF], in1=hsel[:, :, 1 : HALF + 1])
-            nc.vector.tensor_add(out=box[:], in0=box[:], in1=hsel[:, :, 2 : HALF + 2])
-            nc.vector.scalar_tensor_tensor(
-                out=dev[:], in0=box[:, 0, :], scalar=1.0 / NPATCH, in1=box[:, 0, :], op0=ALU.mult, op1=ALU.mult
-            )
-            nc.vector.tensor_sub(out=dev[:], in0=box[:, 1, :], in1=dev[:])
+            b = box[:].rearrange("p (r s) -> p s r", s=2)
+            nc.vector.tensor_scalar_mul(out=mean[:], in0=b[:, 0, :], scalar1=1.0 / NPATCH)
+            nc.vector.tensor_mul(out=dev[:], in0=b[:, 0, :], in1=mean[:])
+            nc.vector.tensor_sub(out=dev[:], in0=b[:, 1, :], in1=dev[:])
             nc.scalar.activation(out=std[:], in_=dev[:], func=ACT.Sqrt, scale=1.0 / (NPATCH - 1))
-            nc.vector.tensor_scalar_mul(out=mean[:], in0=box[:, 0, :], scalar1=1.0 / NPATCH)
 
         def inverse_std():
             nc.vector.reciprocal(out=rstd[:], in_=std[:])
@@ -289,8 +293,9 @@ def tile_norm_conv_kernel(tc, a, conv_kernel, out):
                     in_=res[:].rearrange("p x r j -> p x (r j)"),
                 )
 
-        channel_sums(0, 4)
-        channel_sums(4, 8)
+        gram_matrices(0)
+        gram_matrices(1)
+        channel_sums()
         regroup_a(0)
         squares(0)
         regroup_a(1)
@@ -299,16 +304,16 @@ def tile_norm_conv_kernel(tc, a, conv_kernel, out):
         nc.vector.tensor_copy(out=sums[:, :, 0], in_=s1p[:, :, 0])
         regroup_w("scalar", 2, 0)
         regroup_w("scalar", 2, 1)
-        forward(0)
-        forward(1)
-        row_sums()
-        take_forward(0)
-        take_forward(1)
-        for g in (2, 3):
+        for g in range(4):
             forward(g)
+        for g in range(3):
             take_forward(g)
+        box_sums()
+        regroup_w("vector", 0, 0)
         mean_and_std()
+        quantise_w(2, 0)
         inverse_std()
+        take_forward(3)
         for g in (4, 5):
             forward(g)
             take_forward(g)
@@ -323,18 +328,16 @@ def tile_norm_conv_kernel(tc, a, conv_kernel, out):
         normalise(0, 4, 1, 3)
         backward(1)
         take(1)
-        regroup_w("vector", 0, 0)
+        regroup_w("vector", 1, 0)
         backward(2)
         forward(8)
         take(2)
         take_forward(8)
-        regroup_w("vector", 1, 0)
         normalise(4, 8, 0, 1)
         backward(3)
         take(3)
         quantise_w(0, 0)
         quantise_w(1, 0)
-        quantise_w(2, 0)
         quantise(0)
         normalise(4, 8, 1, 3)
         backward(4)

@@ -359,17 +359,17 @@ def tile_norm_conv_kernel(tc, a, conv_kernel, out):
         forward(10)
         forward(11)
         multiply(1, 0)
+        forward(12)
         take_forward(9)
         take_forward(10)
         take_forward(11)
+        take_forward(12)
         regroup_w("vector", 6, 0)
+        forward(13)
+        take_forward(13)
         quantise(2)
         quantise(4)
         multiply(4, 0)
-        forward(12)
-        forward(13)
-        take_forward(12)
-        take_forward(13)
         quantise_w(6, 0)
         quantise_w(7, 0)
         quantise(5)
@@ -400,17 +400,17 @@ def tile_norm_conv_kernel(tc, a, conv_kernel, out):
         regroup_w("vector", 7, 1)
         quantise_w(5, 1)
         multiply(1, 1)
+        backward(8)
         multiply(4, 1)
+        take(8)
         quantise_w(6, 1)
         quantise_w(7, 1)
         quantise(6)
         quantise_w(8, 1)
         multiply(2, 1)
         multiply(5, 1)
-        backward(8)
         store(0, 1)
         store(1, 1)
-        take(8)
         normalise(12, 13, 0, 3)
         multiply(6, 0)
         normalise(13, 16, 0, 3)

import concourse.mybir as mybir
from concourse.masks import make_identity

F32 = mybir.dt.float32
BF16 = mybir.dt.bfloat16
U32 = mybir.dt.uint32
U8 = mybir.dt.uint8
FP8X4 = mybir.dt.float8_e4m3fn_x4
ALU = mybir.AluOpType
ACT = mybir.ActivationFunctionType
AX = mybir.AxisListType

P = 128
PACK = 4
C = 512
H = 32
W = 32
O = 512
TAPS = 9
NPATCH = C * TAPS
PIX = H * W
HALF = H // 2
BLK_PAIRS = 4
BLK_PIX = BLK_PAIRS * 2 * W
N_BLOCKS = HALF // BLK_PAIRS
N_UNITS = 3 * N_BLOCKS
LAG = 3
TILE = 2 * P
N_FORWARD = (HALF + 2) * 3
PER_BANK = 4
SCALAR_ROWS = 12
OH = O // 2
FLOPS = 2 * PIX * NPATCH * O


def forward_groups(block):
    last_pair = block * BLK_PAIRS + BLK_PAIRS - 1
    return (3 * last_pair + TAPS - 1) // PER_BANK + 1


def tile_norm_conv_kernel(tc, a, conv_kernel, out):
    nc = tc.nc
    a_v = a.rearrange("b (m t) h w -> m (b t) (h w)", t=PACK)
    w_v = conv_kernel.rearrange("(m t k) o -> m t (k o)", t=PACK, k=TAPS)
    out_v = out.rearrange("b (g p) (x r) w -> p (b g) x (r w)", p=P, x=2)

    with tc.tile_pool(name="keep", bufs=1) as keep, tc.tile_pool(name="nrmp", bufs=2) as nrmp, tc.tile_pool(
        name="grpp", bufs=4
    ) as grpp, tc.tile_pool(name="codep", bufs=8) as codep, tc.tile_pool(name="wgp", bufs=8) as wgp, tc.tile_pool(name="resp", bufs=4) as resp, tc.psum_pool(
        name="psum", bufs=1
    ) as psum, tc.manual_schedule():
        ident_f = keep.tile([P, P], F32, name="ident_f")
        make_identity(nc, ident_f[:])
        ones2 = keep.tile([P, 2], BF16, name="ones2")
        nc.vector.memset(ones2[:], 1.0)
        warm = keep.tile([P, 1], F32, name="warm")
        nc.vector.memset(warm[:], 1.0)
        nc.scalar.activation(out=warm[:], in_=warm[:], func=ACT.Sqrt)

        pix_a = (HALF + 1) * W
        a_raw = keep.tile([P, PACK, PIX], BF16, name="a_raw")
        nc.sync.dma_start(out=a_raw[:, :, 0:pix_a], in_=a_v[:, :, 0:pix_a])
        nc.sync.dma_start(out=a_raw[:, :, pix_a:PIX], in_=a_v[:, :, pix_a:PIX])
        w_raw = [keep.tile([P, PACK, 3 * O], BF16, name="w_raw%d" % kh) for kh in range(3)]
        for tap in (2, 0, 1):
            nc.sync.dma_start(out=w_raw[0][:, :, tap * O : (tap + 1) * O], in_=w_v[:, :, tap * O : (tap + 1) * O])
        for kh in (1, 2):
            nc.sync.dma_start(out=w_raw[kh][:], in_=w_v[:, :, kh * 3 * O : (kh + 1) * 3 * O])

        is_q = keep.tile([P, 4], F32, name="is_q")
        nc.vector.tensor_reduce(
            out=is_q[:], in_=ident_f[:].rearrange("p (q j) -> p q j", j=W), axis=AX.X, op=ALU.add
        )
        eye = keep.tile([P, W], F32, name="eye")
        nc.vector.tensor_reduce(out=eye[:], in_=ident_f[:].rearrange("p (q j) -> p j q", j=W), axis=AX.X, op=ALU.add)
        band = keep.tile([P, W], F32, name="band")
        nc.vector.tensor_copy(out=band[:], in_=eye[:])
        nc.vector.tensor_add(out=band[:, 1:W], in0=band[:, 1:W], in1=eye[:, 0 : W - 1])
        nc.vector.tensor_add(out=band[:, 0 : W - 1], in0=band[:, 0 : W - 1], in1=eye[:, 1:W])
        nc.vector.tensor_add(out=band[:, 0:1], in0=band[:, 0:1], in1=eye[:, 1:2])
        nc.vector.tensor_add(out=band[:, W - 1 : W], in0=band[:, W - 1 : W], in1=eye[:, W - 2 : W - 1])
        spread = keep.tile([P, 2, W, 2, 2], F32, name="spread")
        nc.vector.memset(spread[:].rearrange("p s j x u -> p (s j x u)"), 0.0)
        for x in range(2):
            nc.vector.tensor_copy(out=spread[:, x, :, x, :], in_=band[:].unsqueeze(2).to_broadcast([P, W, 2]))

        a_gp = keep.tile([P, HALF + 2, W + 2, 2, PACK], BF16, name="a_gp")
        a_rjt = a_raw[:].rearrange("p t (r j) -> p r j t", j=W)
        a_t = keep.tile([P, N_FORWARD * TILE], BF16, name="a_t")
        sums = keep.tile([P, 8, 2], F32, name="sums")
        diag = keep.tile([P, 2, P], F32, name="diag")
        own = keep.tile([P, H + 2, 2], F32, name="own")
        three = keep.tile([P, H, 2], F32, name="three")
        mean = keep.tile([P, HALF], F32, name="mean")
        dev = keep.tile([P, HALF], F32, name="dev")
        std = keep.tile([P, HALF], F32, name="std")
        rstd = keep.tile([P, HALF], F32, name="rstd")
        w_codes = keep.tile([P, TAPS, O], U32, name="w_codes", align_bytes=64)
        w_scales = keep.tile([P, TAPS, O], U8, name="w_scales", align_bytes=64)

        gram = [psum.tile([P, 4, P], F32, name="gram%d" % h, tag="bk%d" % h) for h in range(2)]
        s1p = psum.tile([P, 8, 2], F32, name="s1p", tag="bk2")
        box = psum.tile([P, 2 * HALF], F32, name="box", tag="bk3")
        state = {"tp": 0}

        def transpose_bank(name):
            bank = 4 + state["tp"] % 4
            state["tp"] = state["tp"] + 1
            return psum.tile([P, PER_BANK * P], F32, name=name, tag="bk%d" % bank)

        def gram_matrices(h):
            for b in range(4 * h, 4 * h + 4):
                for t in range(PACK):
                    slab = a_raw[:, t, b * P : (b + 1) * P]
                    nc.tensor.matmul(
                        out=gram[h][:, b % 4, :], lhsT=slab, rhs=slab, start=(t == 0), stop=(t == PACK - 1)
                    )

        def channel_sums():
            for b in range(8):
                for t in range(PACK):
                    slab = a_raw[:, t, b * P : (b + 1) * P]
                    nc.tensor.matmul(out=s1p[:, b, :], lhsT=slab, rhs=ones2[:], start=(t == 0), stop=(t == PACK - 1))

        def regroup_a(x):
            if x == 0:
                nc.vector.tensor_copy(out=a_gp[:, 1 : HALF + 1, 1 : W + 1, 0, :], in_=a_rjt[:, 0:HALF, :, :])
                nc.vector.tensor_copy(out=a_gp[:, HALF + 1, 1 : W + 1, 0, :], in_=a_rjt[:, HALF, :, :])
                nc.vector.tensor_copy(out=a_gp[:, 0, 1 : W + 1, 0, :], in_=a_rjt[:, 1, :, :])
            else:
                mid = HALF - SCALAR_ROWS
                nc.vector.tensor_copy(out=a_gp[:, 1 : mid + 1, 1 : W + 1, 1, :], in_=a_rjt[:, HALF : HALF + mid, :, :])
                nc.scalar.copy(out=a_gp[:, mid + 1 : HALF + 1, 1 : W + 1, 1, :], in_=a_rjt[:, HALF + mid : H, :, :])
                nc.vector.tensor_copy(out=a_gp[:, 0, 1 : W + 1, 1, :], in_=a_rjt[:, HALF - 1, :, :])
                nc.vector.tensor_copy(out=a_gp[:, HALF + 1, 1 : W + 1, 1, :], in_=a_rjt[:, H - 2, :, :])

        def pad_columns():
            nc.vector.tensor_copy(out=a_gp[:, :, 0 : W + 2 : W + 1, :, :], in_=a_gp[:, :, 2 : W : W - 3, :, :])

        def squares(h):
            for b in range(4 * h, 4 * h + 4):
                nc.vector.scalar_tensor_tensor(
                    out=diag[:, b % 2, :],
                    in0=gram[h][:, b % 4, :],
                    scalar=1.0,
                    in1=ident_f[:],
                    op0=ALU.mult,
                    op1=ALU.mult,
                    accum_out=sums[:, b, 1:2],
                )

        def box_sums():
            nc.vector.tensor_tensor(
                out=own[:, 1 : H + 1, :].rearrange("p (b q) s -> p b q s", q=4),
                in0=sums[:].unsqueeze(2).to_broadcast([P, 8, 4, 2]),
                in1=is_q[:].unsqueeze(1).unsqueeze(3).to_broadcast([P, 8, 4, 2]),
                op=ALU.mult,
            )
            nc.vector.tensor_scalar_mul(out=own[:, 0, :], in0=sums[:, 0, :], scalar1=is_q[:, 1:2])
            nc.vector.tensor_scalar_mul(out=own[:, H + 1, :], in0=sums[:, 7, :], scalar1=is_q[:, 2:3])
            nc.vector.tensor_add(out=three[:], in0=own[:, 0:H, :], in1=own[:, 1 : H + 1, :])
            nc.vector.tensor_add(out=three[:], in0=three[:], in1=own[:, 2 : H + 2, :])
            for x in range(2):
                nc.tensor.matmul(
                    out=box[:],
                    lhsT=spread[:, x, :, :, :].rearrange("p j x u -> p (j x u)"),
                    rhs=three[:, x * HALF : (x + 1) * HALF, :].rearrange("p r s -> p (r s)"),
                    start=(x == 0),
                    stop=(x == 1),
                )

        def mean_and_std():
            b = box[:].rearrange("p (r s) -> p s r", s=2)
            nc.vector.tensor_scalar_mul(out=mean[:], in0=b[:, 0, :], scalar1=1.0 / NPATCH)
            nc.vector.tensor_mul(out=dev[:], in0=b[:, 0, :], in1=mean[:])
            nc.vector.tensor_sub(out=dev[:], in0=b[:, 1, :], in1=dev[:])
            nc.scalar.activation(out=std[:], in_=dev[:], func=ACT.Sqrt, scale=1.0 / (NPATCH - 1))

        def inverse_std():
            nc.vector.reciprocal(out=rstd[:], in_=std[:])

        ahead = {}

        def forward(g):
            first = g * PER_BANK
            ahead[g] = transpose_bank("pt")
            for k in range(min(PER_BANK, N_FORWARD - first)):
                s, kw = divmod(first + k, 3)
                nc.tensor.transpose(
                    ahead[g][:, k * P : (k + 1) * P],
                    a_gp[:, s, kw : kw + W, :, :].rearrange("p j x t -> p (j x t)").bitcast(F32),
                    ident_f[:],
                )

        def take_forward(g):
            first = g * PER_BANK
            cnt = min(PER_BANK, N_FORWARD - first)
            nc.scalar.copy(out=a_t[:, first * TILE : (first + cnt) * TILE].bitcast(F32), in_=ahead[g][:, 0 : cnt * P])

        wg = {}

        def regroup_w(engine, tap, oh):
            wg[tap, oh] = wgp.tile([P, OH * PACK], BF16, name="wg", align_bytes=64)
            kh, kw = divmod(tap, 3)
            first = kw * O + oh * OH
            src = w_raw[kh][:, :, first : first + OH].rearrange("p t (c i) -> p c t i", i=4)
            dst = wg[tap, oh][:].rearrange("p (c i t) -> p c t i", i=4, t=PACK)
            if engine == "vector":
                nc.vector.tensor_copy(out=dst, in_=src)
            else:
                nc.scalar.copy(out=dst, in_=src)

        def quantise_w(tap, oh):
            half = slice(oh * OH, (oh + 1) * OH)
            nc.vector.quantize_mx(
                out=w_codes[:, tap, half].bitcast(FP8X4), scales=w_scales[:, tap, half], in_=wg[tap, oh][:]
            )

        nrm = {}

        def normalise(r0, r1, kh0, kh1):
            for r in range(r0, r1):
                block, rr = divmod(r, BLK_PAIRS)
                if block not in nrm:
                    nrm[block] = nrmp.tile([P, BLK_PAIRS, TAPS * TILE], BF16, name="nrm")
                nc.vector.tensor_scalar(
                    out=nrm[block][:, rr, kh0 * 3 * TILE : kh1 * 3 * TILE],
                    in0=a_t[:, (r + kh0) * 3 * TILE : (r + kh1) * 3 * TILE],
                    scalar1=mean[:, r : r + 1],
                    scalar2=rstd[:, r : r + 1],
                    op0=ALU.subtract,
                    op1=ALU.mult,
                )

        back = {}
        grp = {}
        codes = {}
        scales = {}

        def backward(unit):
            block, kh = divmod(unit, 3)
            for i in range(3):
                tap = kh * 3 + i
                back[unit, i] = transpose_bank("pb")
                for rr in range(BLK_PAIRS):
                    nc.tensor.transpose(
                        back[unit, i][:, rr * P : (rr + 1) * P],
                        nrm[block][:, rr, tap * TILE : (tap + 1) * TILE].bitcast(F32),
                        ident_f[:],
                    )

        def take(unit):
            grp[unit] = grpp.tile([P, 3, BLK_PIX * PACK], BF16, name="grp", align_bytes=64)
            for i in range(3):
                nc.scalar.copy(out=grp[unit][:, i, :].bitcast(F32), in_=back[unit, i][:])

        def quantise(unit):
            codes[unit] = codep.tile([P, 3, BLK_PIX], U32, name="codes", align_bytes=64)
            scales[unit] = codep.tile([P, 3, BLK_PIX], U8, name="scales", align_bytes=64)
            for t0, t1 in ((0, 2), (2, 3)):
                nc.vector.quantize_mx(
                    out=codes[unit][:, t0:t1, :].rearrange("p a b -> p (a b)").bitcast(FP8X4),
                    scales=scales[unit][:, t0:t1, :].rearrange("p a b -> p (a b)"),
                    in_=grp[unit][:, t0:t1, :].rearrange("p a b -> p (a b)"),
                )

        acc = {}

        def multiply(unit, oh):
            block, kh = divmod(unit, 3)
            for ot in (2 * oh, 2 * oh + 1):
                if kh == 0:
                    bank = ot % 2 + 2 * (block if block < 2 else oh)
                    acc[block, ot] = psum.tile([P, BLK_PIX], F32, name="acc", tag="bk%d" % bank)
                for i in range(3):
                    tap = kh * 3 + i
                    nc.tensor.matmul_mx(
                        out=acc[block, ot][:],
                        lhsT=w_codes[:, tap, ot * P : (ot + 1) * P].bitcast(FP8X4),
                        lhsT_scale=w_scales[:, tap, ot * P : (ot + 1) * P],
                        rhs=codes[unit][:, i, :].bitcast(FP8X4),
                        rhs_scale=scales[unit][:, i, :],
                        start=(tap == 0),
                        stop=(tap == TAPS - 1),
                    )

        def store(block, oh):
            for ot in (2 * oh, 2 * oh + 1):
                res = resp.tile([P, 2, BLK_PAIRS, W], F32, name="res")
                nc.scalar.copy(out=res[:], in_=acc[block, ot][:].rearrange("p (r j x) -> p x r j", j=W, x=2))
                nc.sync.dma_start(
                    out=out_v[:, ot, :, block * BLK_PAIRS * W : (block + 1) * BLK_PAIRS * W],
                    in_=res[:].rearrange("p x r j -> p x (r j)"),
                )

        gram_matrices(0)
        gram_matrices(1)
        channel_sums()
        regroup_a(0)
        squares(0)
        regroup_a(1)
        pad_columns()
        squares(1)
        nc.vector.tensor_copy(out=sums[:, :, 0], in_=s1p[:, :, 0])
        regroup_w("scalar", 2, 0)
        regroup_w("scalar", 2, 1)
        for g in range(4):
            forward(g)
        for g in range(3):
            take_forward(g)
        box_sums()
        regroup_w("vector", 0, 0)
        mean_and_std()
        quantise_w(2, 0)
        inverse_std()
        take_forward(3)
        for g in (4, 5):
            forward(g)
            take_forward(g)
        forward(6)
        forward(7)
        take_forward(6)
        take_forward(7)
        normalise(0, 4, 0, 1)
        backward(0)
        take(0)
        regroup_w("scalar", 5, 0)
        normalise(0, 4, 1, 3)
        backward(1)
        take(1)
        regroup_w("vector", 1, 0)
        backward(2)
        forward(8)
        take(2)
        take_forward(8)
        normalise(4, 8, 0, 1)
        backward(3)
        take(3)
        quantise_w(0, 0)
        quantise_w(1, 0)
        quantise(0)
        normalise(4, 8, 1, 3)
        backward(4)
        multiply(0, 0)
        take(4)
        regroup_w("scalar", 7, 0)
        regroup_w("vector", 3, 0)
        backward(5)
        regroup_w("vector", 4, 0)
        quantise(1)
        take(5)
        regroup_w("scalar", 8, 0)
        quantise_w(3, 0)
        quantise_w(4, 0)
        quantise_w(5, 0)
        quantise(3)
        multiply(3, 0)
        forward(9)
        forward(10)
        forward(11)
        multiply(1, 0)
        forward(12)
        take_forward(9)
        take_forward(10)
        take_forward(11)
        take_forward(12)
        regroup_w("vector", 6, 0)
        forward(13)
        take_forward(13)
        quantise(2)
        quantise(4)
        multiply(4, 0)
        quantise_w(6, 0)
        quantise_w(7, 0)
        quantise(5)
        normalise(8, 12, 0, 3)
        backward(6)
        take(6)
        quantise_w(8, 0)
        multiply(2, 0)
        multiply(5, 0)
        backward(7)
        store(0, 0)
        regroup_w("scalar", 5, 1)
        store(1, 0)
        take(7)
        regroup_w("scalar", 8, 1)
        regroup_w("vector", 0, 1)
        regroup_w("vector", 1, 1)
        quantise_w(0, 1)
        quantise_w(1, 1)
        quantise_w(2, 1)
        multiply(0, 1)
        multiply(3, 1)
        regroup_w("vector", 3, 1)
        regroup_w("vector", 4, 1)
        quantise_w(3, 1)
        quantise_w(4, 1)
        regroup_w("vector", 6, 1)
        regroup_w("vector", 7, 1)
        quantise_w(5, 1)
        multiply(1, 1)
        backward(8)
        multiply(4, 1)
        take(8)
        quantise_w(6, 1)
        quantise_w(7, 1)
        quantise(6)
        quantise_w(8, 1)
        multiply(2, 1)
        multiply(5, 1)
        store(0, 1)
        store(1, 1)
        normalise(12, 13, 0, 3)
        multiply(6, 0)
        normalise(13, 16, 0, 3)
        backward(9)
        multiply(6, 1)
        take(9)
        quantise(7)
        multiply(7, 0)
        backward(10)
        multiply(7, 1)
        take(10)
        quantise(8)
        multiply(8, 0)
        multiply(8, 1)
        backward(11)
        store(2, 0)
        store(2, 1)
        take(11)
        quantise(9)
        multiply(9, 0)
        multiply(9, 1)
        quantise(10)
        multiply(10, 0)
        multiply(10, 1)
        quantise(11)
        multiply(11, 0)
        multiply(11, 1)
        store(3, 0)
        store(3, 1)
